import numpy as np
import ml_dtypes


def mxq(x, axis, fmt="e4m3"):
    dtype, down = {"e4m3": (ml_dtypes.float8_e4m3fn, 7), "e5m2": (ml_dtypes.float8_e5m2, 14)}[fmt]
    v = np.moveaxis(np.asarray(x, np.float32).astype(ml_dtypes.bfloat16).astype(np.float64), axis, -1)
    blocks = v.reshape(v.shape[:-1] + (-1, 32))
    amax = np.abs(blocks).max(-1, keepdims=True)
    byte = np.maximum(np.where(amax > 0, np.frexp(amax)[1] - 1 + 127, 0) - down, 1)
    scale = np.exp2(byte - 127.0)
    codes = (blocks / scale).astype(np.float32).astype(dtype).astype(np.float64)
    return np.moveaxis((codes * scale).reshape(v.shape), -1, axis)


WIDE = False


def mx_kscale(k):
    if not WIDE:
        return np.ones(k)
    levels = np.array([10, -10, 5, -5, 0])
    a = np.random.permutation(np.resize(levels, k // 512 * 4)).reshape(k // 512, 4)
    idx = np.arange(k)
    return np.exp2(a[idx // 512, idx % 128 // 32])


BF16 = ml_dtypes.bfloat16


def bf(x):
    return np.asarray(x, np.float32).astype(BF16)


def f64(x):
    return np.asarray(x).astype(np.float64)


E2M1 = np.array([0.0, 0.5, 1.0, 1.5, 2.0, 3.0, 4.0, 6.0, -0.0, -0.5, -1.0, -1.5, -2.0, -3.0, -4.0, -6.0])


def pack_weight(w, fmt):
    k, n = w.shape
    w = f64(bf(w)).reshape(k // 32, 32, n)
    amax = np.abs(w).max(1)
    if fmt == "e4m3":
        byte = np.frexp(amax)[1] - 1 + 127 - 7
    else:
        mant, ex = np.frexp(amax / 6.0)
        byte = np.where(mant > 0.5, ex, ex - 1) + 127
    byte = np.clip(np.where(amax > 0, byte, 1), 1, 254)
    scaled = (w * np.exp2(127.0 - byte)[:, None, :]).reshape(k, n).astype(np.float32)
    by_word = np.ascontiguousarray(scaled.reshape(k // 512, 128, 4, n).transpose(0, 1, 3, 2))
    if fmt == "e4m3":
        words = by_word.astype(ml_dtypes.float8_e4m3fn).view(np.uint8)
    else:
        c = by_word.astype(ml_dtypes.float4_e2m1fn).view(np.uint8) & 0xF
        words = c[..., 0::2] | (c[..., 1::2] << 4)
    return np.ascontiguousarray(words), np.ascontiguousarray(byte.astype(np.uint8).reshape(k // 512, 16, n))


def unpack_weight(words, scales, fmt):
    g, p, n, _ = words.shape
    if fmt == "e4m3":
        vals = np.ascontiguousarray(words).view(ml_dtypes.float8_e4m3fn).astype(np.float64)
    else:
        nib = np.empty((g, p, n, 4), np.uint8)
        nib[..., 0::2] = words & 0xF
        nib[..., 1::2] = words >> 4
        vals = E2M1[nib]
    vals = vals * np.repeat(np.exp2(scales.astype(np.float64) - 127.0), 8, axis=1)[..., None]
    return vals.transpose(0, 1, 3, 2).reshape(g * 512, n)

def pack4(w):
    words, scales = pack_weight(w, "e2m1")
    return words.reshape(words.shape[0], 128, -1), scales


def unpack4(words, scales):
    return unpack_weight(words.reshape(words.shape[0], 128, -1, 2), scales, "e2m1")


S, HID, H, KV, D, WINDOW, QB = 4096, 1024, 4, 2, 128, 512, 512
NQ, NK = H * D, KV * D
EPS = 1e-6
ROPE_THETA = 10000.0


def rms_norm(x, w):
    var = np.mean(x * x, axis=-1, keepdims=True)
    return x * (1.0 / np.sqrt(var + EPS)) * (1.0 + w)


def rotate_half(x):
    x1, x2 = np.split(x, 2, axis=-1)
    return np.concatenate([-x2, x1], axis=-1)


def apply_rope(x, cos, sin):
    return x * cos[:, None, :] + rotate_half(x) * sin[:, None, :]


def setup_inputs():
    s = mx_kscale(HID)
    inv_freq = 1.0 / ROPE_THETA ** (np.arange(0, D, 2) / D)
    freqs = np.outer(np.arange(S), inv_freq)
    emb = np.concatenate([freqs, freqs], -1)
    hidden_states = bf(np.random.standard_normal((S, HID)) * s)
    words, scales = pack4(np.random.standard_normal((HID, NQ + NK + NK)) / np.sqrt(HID) / s[:, None])
    return {"hidden_states": hidden_states,
            "w_qkv_words": words, "w_qkv_scales": scales,
            "q_norm_w": bf(1.0 + 0.1 * np.random.standard_normal(D)),
            "k_norm_w": bf(1.0 + 0.1 * np.random.standard_normal(D)),
            "cos": bf(np.cos(emb)), "sin": bf(np.sin(emb))}


def reference(hidden_states, w_qkv_words, w_qkv_scales, q_norm_w, k_norm_w, cos, sin):
    qkv = mxq(f64(hidden_states), 1, "e4m3") @ unpack4(w_qkv_words, w_qkv_scales)
    q = qkv[:, :NQ].reshape(S, H, D)
    k = qkv[:, NQ:NQ + NK].reshape(S, KV, D)
    v = qkv[:, NQ + NK:].reshape(S, KV, D)
    q = rms_norm(q, f64(q_norm_w))
    k = rms_norm(k, f64(k_norm_w))
    q = apply_rope(q, f64(cos), f64(sin))
    k = apply_rope(k, f64(cos), f64(sin))
    return q, k, v

@@ -1,0 +1,239 @@
+from contextlib import ExitStack
+
+import concourse.mybir as mybir
+from concourse.masks import make_identity
+
+F32 = mybir.dt.float32
+BF16 = mybir.dt.bfloat16
+I32 = mybir.dt.int32
+U8 = mybir.dt.uint8
+U32 = mybir.dt.uint32
+FP8X4 = mybir.dt.float8_e4m3fn_x4
+FP4X4 = mybir.dt.float4_e2m1fn_x4
+ALU = mybir.AluOpType
+ACT = mybir.ActivationFunctionType
+
+P = 128
+S = 4096
+HID = 1024
+D = 128
+HALF = D // 2
+Q_HEADS = 4
+K_HEADS = 2
+V_HEADS = 2
+NORMED = Q_HEADS + K_HEADS
+N_OUT = (Q_HEADS + K_HEADS + V_HEADS) * D
+N_PASS = 512
+K_PASS = 512
+PASSES = HID // K_PASS
+TILES = S // P
+CHUNK = 4
+CHUNKS = TILES // CHUNK
+PAIR = 2
+AHEAD = 2
+EPS = 1e-6
+
+FLOPS = 2 * S * HID * N_OUT
+
+
+def tile_gemmaattention_pa_t_kernel(
+    tc, hidden_states, w_qkv_words, w_qkv_scales, q_norm_w, k_norm_w, cos, sin, out_0, out_1, out_2
+):
+    nc = tc.nc
+    x_dram = hidden_states.rearrange("(p t) k -> p t k", t=TILES)
+    cos_dram = cos.rearrange("(p t) d -> p t d", t=TILES)
+    sin_dram = sin.rearrange("(p t) d -> p t d", t=TILES)
+    q_dram = out_0.rearrange("(p t) h d -> p t (h d)", t=TILES)
+    k_dram = out_1.rearrange("(p t) h d -> p t (h d)", t=TILES)
+    v_dram = out_2.rearrange("(p t) h d -> p t (h d)", t=TILES)
+
+    with ExitStack() as ctx:
+        keep = ctx.enter_context(tc.tile_pool(name="keep", bufs=1))
+        tables = ctx.enter_context(tc.tile_pool(name="tables", bufs=3))
+        front = ctx.enter_context(tc.tile_pool(name="front", bufs=3))
+        work = ctx.enter_context(tc.tile_pool(name="work", bufs=3))
+        outs = ctx.enter_context(tc.tile_pool(name="outs", bufs=3))
+        psum_keep = ctx.enter_context(tc.psum_pool(name="psum_keep", bufs=1))
+        psum_t = ctx.enter_context(tc.psum_pool(name="psum_t", bufs=3))
+        psum_acc = ctx.enter_context(tc.psum_pool(name="psum_acc", bufs=2))
+
+        x_sb = []
+        for c in range(CHUNKS):
+            x_sb.append(keep.tile([P, CHUNK, HID], BF16, name="x%d" % c))
+        w_planes = keep.tile([P, PASSES, N_OUT], U8, align_bytes=64)
+        w_words = keep.tile([P, PASSES, 2 * N_OUT], U8, align_bytes=64)
+        norm_w = keep.tile([P, 2, D], BF16)
+        cos_sb = keep.tile([P, TILES, D], BF16)
+        sin_sb = keep.tile([P, TILES, D], BF16)
+
+        nc.vector.memset(w_planes[:].bitcast(I32), 0)
+        nc.vector.memset(norm_w[:], 0.0)
+
+        nc.sync.dma_start(out=x_sb[0][:, 0:PAIR, :], in_=x_dram[:, 0:PAIR, :])
+        scale_rows = w_qkv_scales.bitcast(I32).rearrange("g (q r) n -> r q g n", r=4)
+        for r in range(4):
+            nc.sync.dma_start(out=w_planes[r:P:32, :, :].bitcast(I32), in_=scale_rows[r])
+        nc.sync.dma_start(
+            out=w_words[:].bitcast(I32), in_=w_qkv_words.bitcast(I32).rearrange("g p b -> p g b")
+        )
+        nc.sync.dma_start(out=norm_w[0:1, 0, :], in_=q_norm_w.unsqueeze(0))
+        nc.sync.dma_start(out=norm_w[0:1, 1, :], in_=k_norm_w.unsqueeze(0))
+        nc.sync.dma_start(out=cos_sb[:, 0:CHUNK, :], in_=cos_dram[:, 0:CHUNK, :])
+        nc.sync.dma_start(out=sin_sb[:, 0:CHUNK, :], in_=sin_dram[:, 0:CHUNK, :])
+        nc.sync.dma_start(out=x_sb[0][:, PAIR:CHUNK, :], in_=x_dram[:, PAIR:CHUNK, :])
+        nc.sync.dma_start(out=cos_sb[:, CHUNK:TILES, :], in_=cos_dram[:, CHUNK:TILES, :])
+        nc.sync.dma_start(out=sin_sb[:, CHUNK:TILES, :], in_=sin_dram[:, CHUNK:TILES, :])
+        for c in range(1, CHUNKS):
+            nc.sync.dma_start(out=x_sb[c][:], in_=x_dram[:, c * CHUNK : (c + 1) * CHUNK, :])
+
+        ident = keep.tile([P, P], F32)
+        make_identity(nc, ident[:])
+
+        gain_row = keep.tile([P, 2, 2, D], F32)
+        nc.vector.tensor_scalar(
+            out=gain_row[:, :, 0, :], in0=norm_w[:], scalar1=1.0, scalar2=1.0, op0=ALU.mult, op1=ALU.add
+        )
+        nc.vector.tensor_scalar(
+            out=gain_row[:, :, 1, 0:HALF], in0=norm_w[:, :, 0:HALF],
+            scalar1=1.0, scalar2=1.0, op0=ALU.mult, op1=ALU.add,
+        )
+        nc.vector.tensor_scalar(
+            out=gain_row[:, :, 1, HALF:D], in0=norm_w[:, :, HALF:D],
+            scalar1=-1.0, scalar2=-1.0, op0=ALU.mult, op1=ALU.add,
+        )
+        pick_row0 = keep.tile([P, P], F32)
+        nc.vector.memset(pick_row0[:], 0.0)
+        nc.vector.memset(pick_row0[0:1, :], 1.0)
+        gain_ps = psum_keep.tile([P, 2, 2, D], F32)
+        nc.tensor.matmul(
+            out=gain_ps[:].rearrange("p a b d -> p (a b d)"),
+            lhsT=pick_row0[:],
+            rhs=gain_row[:].rearrange("p a b d -> p (a b d)"),
+            start=True,
+            stop=True,
+        )
+        gain_sb = keep.tile([P, 2, 2, D], F32)
+        nc.scalar.copy(out=gain_sb[:], in_=gain_ps[:])
+
+        def make_tables(c):
+            table = tables.tile([P, CHUNK, 2, 2, D], F32, name="table")
+            ts = slice(c * CHUNK, (c + 1) * CHUNK)
+            low = slice(0, HALF)
+            high = slice(HALF, D)
+            nc.vector.tensor_tensor(
+                out=table[:, :, :, 0, :],
+                in0=gain_ps[:, :, 0, :].unsqueeze(1).to_broadcast([P, CHUNK, 2, D]),
+                in1=cos_sb[:, ts, :].unsqueeze(2).to_broadcast([P, CHUNK, 2, D]),
+                op=ALU.mult,
+            )
+            nc.vector.tensor_tensor(
+                out=table[:, :, :, 1, low],
+                in0=gain_ps[:, :, 1, low].unsqueeze(1).to_broadcast([P, CHUNK, 2, HALF]),
+                in1=sin_sb[:, ts, high].unsqueeze(2).to_broadcast([P, CHUNK, 2, HALF]),
+                op=ALU.mult,
+            )
+            nc.gpsimd.tensor_tensor(
+                out=table[:, :, :, 1, high],
+                in0=gain_sb[:, :, 1, high].unsqueeze(1).to_broadcast([P, CHUNK, 2, HALF]),
+                in1=sin_sb[:, ts, low].unsqueeze(2).to_broadcast([P, CHUNK, 2, HALF]),
+                op=ALU.mult,
+            )
+            return table
+
+        def transpose_and_quantise(t):
+            x_words = x_sb[t // CHUNK][:, t % CHUNK, :].bitcast(F32)
+            flipped = psum_t.tile([P, 2 * PASSES, P], F32, name="flipped")
+            for g in range(PASSES):
+                for u in range(2):
+                    nc.tensor.transpose(
+                        flipped[:, 2 * g + u, :],
+                        x_words[:, 256 * g + u : 256 * (g + 1) : 2],
+                        ident[:],
+                    )
+            grouped = front.tile([P, PASSES * P * 4], BF16, name="grouped", align_bytes=64)
+            nc.scalar.copy(
+                out=grouped[:].bitcast(F32).rearrange("p (g m u) -> p g m u", g=PASSES, u=2),
+                in_=flipped[:].rearrange("p (g u) m -> p g m u", u=2),
+            )
+            codes = front.tile([P, PASSES * P], U32, name="codes", align_bytes=64)
+            planes = front.tile([P, PASSES * P], U8, name="planes", align_bytes=64)
+            nc.vector.quantize_mx(out=codes[:].bitcast(FP8X4), scales=planes[:], in_=grouped[:])
+            return codes, planes
+
+        def project(codes, planes):
+            banks = []
+            for n in range(N_OUT // N_PASS):
+                acc = psum_acc.tile([P, N_PASS], F32, name="acc%d" % n)
+                for g in range(PASSES):
+                    nc.tensor.matmul_mx(
+                        out=acc[:],
+                        lhsT=codes[:, g * P : (g + 1) * P].bitcast(FP8X4),
+                        lhsT_scale=planes[:, g * P : (g + 1) * P],
+                        rhs=w_words[:, g, 2 * n * N_PASS : 2 * (n + 1) * N_PASS].bitcast(FP4X4),
+                        rhs_scale=w_planes[:, g, n * N_PASS : (n + 1) * N_PASS],
+                        start=(g == 0),
+                        stop=(g == PASSES - 1),
+                    )
+                banks.append(acc)
+            return banks
+
+        def head_columns(banks, h):
+            return banks[h // Q_HEADS][:, (h % Q_HEADS) * D : (h % Q_HEADS + 1) * D]
+
+        state = {}
+        ready = {}
+        for t in range(AHEAD):
+            ready[t] = transpose_and_quantise(t)
+        next_table = make_tables(0)
+
+        for t in range(TILES):
+            i = t % PAIR
+            if t % CHUNK == 0:
+                state["table"] = next_table
+                if t // CHUNK + 1 < CHUNKS:
+                    next_table = make_tables(t // CHUNK + 1)
+            if i == 0:
+                state["prod"] = work.tile([P, PAIR * NORMED, 2, D], F32, name="prod")
+                state["qk_out"] = outs.tile([P, PAIR * NORMED, D], F32, name="qk_out")
+                state["v_out"] = outs.tile([P, PAIR, V_HEADS * D], F32, name="v_out")
+            if t + AHEAD < TILES:
+                ready[t + AHEAD] = transpose_and_quantise(t + AHEAD)
+            codes, planes = ready[t]
+            banks = project(codes, planes)
+
+            squares = work.tile([P, NORMED, D], BF16, name="squares")
+            sumsq = work.tile([P, NORMED], F32, name="sumsq")
+            for h in range(NORMED):
+                nc.scalar.activation(
+                    out=squares[:, h, :], in_=head_columns(banks, h), func=ACT.Square,
+                    accum_out=sumsq[:, h : h + 1],
+                )
+            rstd = work.tile([P, NORMED], F32, name="rstd")
+            nc.scalar.activation(
+                out=rstd[:], in_=sumsq[:], func=ACT.Abs_reciprocal_sqrt, scale=1.0 / D, bias=EPS
+            )
+            nc.scalar.copy(out=state["v_out"][:, i, :], in_=banks[1][:, K_HEADS * D : N_PASS])
+            for h in range(NORMED):
+                nc.vector.scalar_tensor_tensor(
+                    out=state["prod"][:, i * NORMED + h, :, :],
+                    in0=head_columns(banks, h).unsqueeze(1).to_broadcast([P, 2, D]),
+                    scalar=rstd[:, h : h + 1],
+                    in1=state["table"][:, t % CHUNK, h // Q_HEADS, :, :],
+                    op0=ALU.mult,
+                    op1=ALU.mult,
+                )
+            if i == PAIR - 1:
+                for half in range(2):
+                    mine = slice(half * HALF, (half + 1) * HALF)
+                    other = slice((1 - half) * HALF, (2 - half) * HALF)
+                    nc.gpsimd.tensor_tensor(
+                        out=state["qk_out"][:, :, mine],
+                        in0=state["prod"][:, :, 0, mine],
+                        in1=state["prod"][:, :, 1, other],
+                        op=ALU.add,
+                    )
+                ts = slice(t - PAIR + 1, t + 1)
+                by_tile = state["qk_out"][:].rearrange("p (i h) d -> p i (h d)", h=NORMED)
+                nc.sync.dma_start(out=v_dram[:, ts, :], in_=state["v_out"][:])
+                nc.sync.dma_start(out=q_dram[:, ts, :], in_=by_tile[:, :, 0 : Q_HEADS * D])
+                nc.sync.dma_start(out=k_dram[:, ts, :], in_=by_tile[:, :, Q_HEADS * D : NORMED * D])

@@ -54,8 +54,9 @@ def tile_gemmaattention_pa_t_kernel(
         work = ctx.enter_context(tc.tile_pool(name="work", bufs=3))
         outs = ctx.enter_context(tc.tile_pool(name="outs", bufs=3))
         psum_keep = ctx.enter_context(tc.psum_pool(name="psum_keep", bufs=1))
-        psum_t = ctx.enter_context(tc.psum_pool(name="psum_t", bufs=3))
-        psum_acc = ctx.enter_context(tc.psum_pool(name="psum_acc", bufs=2))
+        psum_t = ctx.enter_context(tc.psum_pool(name="psum_t", bufs=2))
+        psum_q = ctx.enter_context(tc.psum_pool(name="psum_q", bufs=3))
+        psum_kv = ctx.enter_context(tc.psum_pool(name="psum_kv", bufs=2))
 
         x_sb = []
         for c in range(CHUNKS):
@@ -88,32 +89,6 @@ def tile_gemmaattention_pa_t_kernel(
 
         ident = keep.tile([P, P], F32)
         make_identity(nc, ident[:])
-
-        gain_row = keep.tile([P, 2, 2, D], F32)
-        nc.vector.tensor_scalar(
-            out=gain_row[:, :, 0, :], in0=norm_w[:], scalar1=1.0, scalar2=1.0, op0=ALU.mult, op1=ALU.add
-        )
-        nc.vector.tensor_scalar(
-            out=gain_row[:, :, 1, 0:HALF], in0=norm_w[:, :, 0:HALF],
-            scalar1=1.0, scalar2=1.0, op0=ALU.mult, op1=ALU.add,
-        )
-        nc.vector.tensor_scalar(
-            out=gain_row[:, :, 1, HALF:D], in0=norm_w[:, :, HALF:D],
-            scalar1=-1.0, scalar2=-1.0, op0=ALU.mult, op1=ALU.add,
-        )
-        pick_row0 = keep.tile([P, P], F32)
-        nc.vector.memset(pick_row0[:], 0.0)
-        nc.vector.memset(pick_row0[0:1, :], 1.0)
-        gain_ps = psum_keep.tile([P, 2, 2, D], F32)
-        nc.tensor.matmul(
-            out=gain_ps[:].rearrange("p a b d -> p (a b d)"),
-            lhsT=pick_row0[:],
-            rhs=gain_row[:].rearrange("p a b d -> p (a b d)"),
-            start=True,
-            stop=True,
-        )
-        gain_sb = keep.tile([P, 2, 2, D], F32)
-        nc.scalar.copy(out=gain_sb[:], in_=gain_ps[:])
 
         def make_tables(c):
             table = tables.tile([P, CHUNK, 2, 2, D], F32, name="table")
@@ -160,30 +135,70 @@ def tile_gemmaattention_pa_t_kernel(
             nc.vector.quantize_mx(out=codes[:].bitcast(FP8X4), scales=planes[:], in_=grouped[:])
             return codes, planes
 
-        def project(codes, planes):
-            banks = []
-            for n in range(N_OUT // N_PASS):
-                acc = psum_acc.tile([P, N_PASS], F32, name="acc%d" % n)
-                for g in range(PASSES):
-                    nc.tensor.matmul_mx(
-                        out=acc[:],
-                        lhsT=codes[:, g * P : (g + 1) * P].bitcast(FP8X4),
-                        lhsT_scale=planes[:, g * P : (g + 1) * P],
-                        rhs=w_words[:, g, 2 * n * N_PASS : 2 * (n + 1) * N_PASS].bitcast(FP4X4),
-                        rhs_scale=w_planes[:, g, n * N_PASS : (n + 1) * N_PASS],
-                        start=(g == 0),
-                        stop=(g == PASSES - 1),
-                    )
-                banks.append(acc)
-            return banks
+        def project(codes, planes, acc, n):
+            for g in range(PASSES):
+                nc.tensor.matmul_mx(
+                    out=acc[:],
+                    lhsT=codes[:, g * P : (g + 1) * P].bitcast(FP8X4),
+                    lhsT_scale=planes[:, g * P : (g + 1) * P],
+                    rhs=w_words[:, g, 2 * n * N_PASS : 2 * (n + 1) * N_PASS].bitcast(FP4X4),
+                    rhs_scale=w_planes[:, g, n * N_PASS : (n + 1) * N_PASS],
+                    start=(g == 0),
+                    stop=(g == PASSES - 1),
+                )
 
-        def head_columns(banks, h):
-            return banks[h // Q_HEADS][:, (h % Q_HEADS) * D : (h % Q_HEADS + 1) * D]
+        def norm_and_products(acc, heads, table, prod):
+            squares = work.tile([P, heads, D], BF16, name="squares%d" % heads)
+            sumsq = work.tile([P, heads], F32, name="sumsq%d" % heads)
+            for h in range(heads):
+                nc.scalar.activation(
+                    out=squares[:, h, :], in_=acc[:, h * D : (h + 1) * D], func=ACT.Square,
+                    accum_out=sumsq[:, h : h + 1],
+                )
+            rstd = work.tile([P, heads], F32, name="rstd%d" % heads)
+            nc.scalar.activation(
+                out=rstd[:], in_=sumsq[:], func=ACT.Abs_reciprocal_sqrt, scale=1.0 / D, bias=EPS
+            )
+            for h in range(heads):
+                nc.vector.scalar_tensor_tensor(
+                    out=prod[:, h, :, :],
+                    in0=acc[:, h * D : (h + 1) * D].unsqueeze(1).to_broadcast([P, 2, D]),
+                    scalar=rstd[:, h : h + 1],
+                    in1=table,
+                    op0=ALU.mult,
+                    op1=ALU.mult,
+                )
 
         state = {}
         ready = {}
         for t in range(AHEAD):
             ready[t] = transpose_and_quantise(t)
+        gain_row = keep.tile([P, 2, 2, D], F32)
+        nc.vector.tensor_scalar(
+            out=gain_row[:, :, 0, :], in0=norm_w[:], scalar1=1.0, scalar2=1.0, op0=ALU.mult, op1=ALU.add
+        )
+        nc.vector.tensor_scalar(
+            out=gain_row[:, :, 1, 0:HALF], in0=norm_w[:, :, 0:HALF],
+            scalar1=1.0, scalar2=1.0, op0=ALU.mult, op1=ALU.add,
+        )
+        nc.vector.tensor_scalar(
+            out=gain_row[:, :, 1, HALF:D], in0=norm_w[:, :, HALF:D],
+            scalar1=-1.0, scalar2=-1.0, op0=ALU.mult, op1=ALU.add,
+        )
+        pick_row0 = keep.tile([P, P], F32)
+        nc.vector.memset(pick_row0[:], 0.0)
+        nc.vector.memset(pick_row0[0:1, :], 1.0)
+        gain_ps = psum_keep.tile([P, 2, 2, D], F32)
+        nc.tensor.matmul(
+            out=gain_ps[:].rearrange("p a b d -> p (a b d)"),
+            lhsT=pick_row0[:],
+            rhs=gain_row[:].rearrange("p a b d -> p (a b d)"),
+            start=True,
+            stop=True,
+        )
+        gain_sb = keep.tile([P, 2, 2, D], F32)
+        nc.scalar.copy(out=gain_sb[:], in_=gain_ps[:])
+
         next_table = make_tables(0)
 
         for t in range(TILES):
@@ -199,29 +214,21 @@ def tile_gemmaattention_pa_t_kernel(
             if t + AHEAD < TILES:
                 ready[t + AHEAD] = transpose_and_quantise(t + AHEAD)
             codes, planes = ready[t]
-            banks = project(codes, planes)
-
-            squares = work.tile([P, NORMED, D], BF16, name="squares")
-            sumsq = work.tile([P, NORMED], F32, name="sumsq")
-            for h in range(NORMED):
-                nc.scalar.activation(
-                    out=squares[:, h, :], in_=head_columns(banks, h), func=ACT.Square,
-                    accum_out=sumsq[:, h : h + 1],
-                )
-            rstd = work.tile([P, NORMED], F32, name="rstd")
-            nc.scalar.activation(
-                out=rstd[:], in_=sumsq[:], func=ACT.Abs_reciprocal_sqrt, scale=1.0 / D, bias=EPS
+            acc_kv = psum_kv.tile([P, N_PASS], F32, name="acc_kv")
+            project(codes, planes, acc_kv, 1)
+            acc_q = psum_q.tile([P, N_PASS], F32, name="acc_q")
+            project(codes, planes, acc_q, 0)
+            first = i * NORMED
+            table = state["table"]
+            nc.scalar.copy(out=state["v_out"][:, i, :], in_=acc_kv[:, K_HEADS * D : N_PASS])
+            norm_and_products(
+                acc_kv, K_HEADS, table[:, t % CHUNK, 1, :, :],
+                state["prod"][:, first + Q_HEADS : first + NORMED, :, :],
             )
-            nc.scalar.copy(out=state["v_out"][:, i, :], in_=banks[1][:, K_HEADS * D : N_PASS])
-            for h in range(NORMED):
-                nc.vector.scalar_tensor_tensor(
-                    out=state["prod"][:, i * NORMED + h, :, :],
-                    in0=head_columns(banks, h).unsqueeze(1).to_broadcast([P, 2, D]),
-                    scalar=rstd[:, h : h + 1],
-                    in1=state["table"][:, t % CHUNK, h // Q_HEADS, :, :],
-                    op0=ALU.mult,
-                    op1=ALU.mult,
-                )
+            norm_and_products(
+                acc_q, Q_HEADS, table[:, t % CHUNK, 0, :, :],
+                state["prod"][:, first : first + Q_HEADS, :, :],
+            )
             if i == PAIR - 1:
                 for half in range(2):
                     mine = slice(half * HALF, (half + 1) * HALF)

@@ -30,7 +30,7 @@ TILES = S // P
 CHUNK = 4
 CHUNKS = TILES // CHUNK
 PAIR = 2
-AHEAD = 2
+FLIP_AHEAD = 6
 EPS = 1e-6
 
 FLOPS = 2 * S * HID * N_OUT
@@ -54,9 +54,8 @@ def tile_gemmaattention_pa_t_kernel(
         work = ctx.enter_context(tc.tile_pool(name="work", bufs=3))
         outs = ctx.enter_context(tc.tile_pool(name="outs", bufs=3))
         psum_keep = ctx.enter_context(tc.psum_pool(name="psum_keep", bufs=1))
-        psum_t = ctx.enter_context(tc.psum_pool(name="psum_t", bufs=2))
-        psum_q = ctx.enter_context(tc.psum_pool(name="psum_q", bufs=3))
-        psum_kv = ctx.enter_context(tc.psum_pool(name="psum_kv", bufs=2))
+        psum_t = ctx.enter_context(tc.psum_pool(name="psum_t", bufs=3))
+        psum_acc = ctx.enter_context(tc.psum_pool(name="psum_acc", bufs=2))
 
         x_sb = []
         for c in range(CHUNKS):
@@ -90,89 +89,6 @@ def tile_gemmaattention_pa_t_kernel(
         ident = keep.tile([P, P], F32)
         make_identity(nc, ident[:])
 
-        def make_tables(c):
-            table = tables.tile([P, CHUNK, 2, 2, D], F32, name="table")
-            ts = slice(c * CHUNK, (c + 1) * CHUNK)
-            low = slice(0, HALF)
-            high = slice(HALF, D)
-            nc.vector.tensor_tensor(
-                out=table[:, :, :, 0, :],
-                in0=gain_ps[:, :, 0, :].unsqueeze(1).to_broadcast([P, CHUNK, 2, D]),
-                in1=cos_sb[:, ts, :].unsqueeze(2).to_broadcast([P, CHUNK, 2, D]),
-                op=ALU.mult,
-            )
-            nc.vector.tensor_tensor(
-                out=table[:, :, :, 1, low],
-                in0=gain_ps[:, :, 1, low].unsqueeze(1).to_broadcast([P, CHUNK, 2, HALF]),
-                in1=sin_sb[:, ts, high].unsqueeze(2).to_broadcast([P, CHUNK, 2, HALF]),
-                op=ALU.mult,
-            )
-            nc.gpsimd.tensor_tensor(
-                out=table[:, :, :, 1, high],
-                in0=gain_sb[:, :, 1, high].unsqueeze(1).to_broadcast([P, CHUNK, 2, HALF]),
-                in1=sin_sb[:, ts, low].unsqueeze(2).to_broadcast([P, CHUNK, 2, HALF]),
-                op=ALU.mult,
-            )
-            return table
-
-        def transpose_and_quantise(t):
-            x_words = x_sb[t // CHUNK][:, t % CHUNK, :].bitcast(F32)
-            flipped = psum_t.tile([P, 2 * PASSES, P], F32, name="flipped")
-            for g in range(PASSES):
-                for u in range(2):
-                    nc.tensor.transpose(
-                        flipped[:, 2 * g + u, :],
-                        x_words[:, 256 * g + u : 256 * (g + 1) : 2],
-                        ident[:],
-                    )
-            grouped = front.tile([P, PASSES * P * 4], BF16, name="grouped", align_bytes=64)
-            nc.scalar.copy(
-                out=grouped[:].bitcast(F32).rearrange("p (g m u) -> p g m u", g=PASSES, u=2),
-                in_=flipped[:].rearrange("p (g u) m -> p g m u", u=2),
-            )
-            codes = front.tile([P, PASSES * P], U32, name="codes", align_bytes=64)
-            planes = front.tile([P, PASSES * P], U8, name="planes", align_bytes=64)
-            nc.vector.quantize_mx(out=codes[:].bitcast(FP8X4), scales=planes[:], in_=grouped[:])
-            return codes, planes
-
-        def project(codes, planes, acc, n):
-            for g in range(PASSES):
-                nc.tensor.matmul_mx(
-                    out=acc[:],
-                    lhsT=codes[:, g * P : (g + 1) * P].bitcast(FP8X4),
-                    lhsT_scale=planes[:, g * P : (g + 1) * P],
-                    rhs=w_words[:, g, 2 * n * N_PASS : 2 * (n + 1) * N_PASS].bitcast(FP4X4),
-                    rhs_scale=w_planes[:, g, n * N_PASS : (n + 1) * N_PASS],
-                    start=(g == 0),
-                    stop=(g == PASSES - 1),
-                )
-
-        def norm_and_products(acc, heads, table, prod):
-            squares = work.tile([P, heads, D], BF16, name="squares%d" % heads)
-            sumsq = work.tile([P, heads], F32, name="sumsq%d" % heads)
-            for h in range(heads):
-                nc.scalar.activation(
-                    out=squares[:, h, :], in_=acc[:, h * D : (h + 1) * D], func=ACT.Square,
-                    accum_out=sumsq[:, h : h + 1],
-                )
-            rstd = work.tile([P, heads], F32, name="rstd%d" % heads)
-            nc.scalar.activation(
-                out=rstd[:], in_=sumsq[:], func=ACT.Abs_reciprocal_sqrt, scale=1.0 / D, bias=EPS
-            )
-            for h in range(heads):
-                nc.vector.scalar_tensor_tensor(
-                    out=prod[:, h, :, :],
-                    in0=acc[:, h * D : (h + 1) * D].unsqueeze(1).to_broadcast([P, 2, D]),
-                    scalar=rstd[:, h : h + 1],
-                    in1=table,
-                    op0=ALU.mult,
-                    op1=ALU.mult,
-                )
-
-        state = {}
-        ready = {}
-        for t in range(AHEAD):
-            ready[t] = transpose_and_quantise(t)
         gain_row = keep.tile([P, 2, 2, D], F32)
         nc.vector.tensor_scalar(
             out=gain_row[:, :, 0, :], in0=norm_w[:], scalar1=1.0, scalar2=1.0, op0=ALU.mult, op1=ALU.add
@@ -199,6 +115,93 @@ def tile_gemmaattention_pa_t_kernel(
         gain_sb = keep.tile([P, 2, 2, D], F32)
         nc.scalar.copy(out=gain_sb[:], in_=gain_ps[:])
 
+        def make_tables(c):
+            table = tables.tile([P, CHUNK, 2, 2, D], F32, name="table")
+            ts = slice(c * CHUNK, (c + 1) * CHUNK)
+            low = slice(0, HALF)
+            high = slice(HALF, D)
+            nc.vector.tensor_tensor(
+                out=table[:, :, :, 0, :],
+                in0=gain_ps[:, :, 0, :].unsqueeze(1).to_broadcast([P, CHUNK, 2, D]),
+                in1=cos_sb[:, ts, :].unsqueeze(2).to_broadcast([P, CHUNK, 2, D]),
+                op=ALU.mult,
+            )
+            nc.vector.tensor_tensor(
+                out=table[:, :, :, 1, low],
+                in0=gain_ps[:, :, 1, low].unsqueeze(1).to_broadcast([P, CHUNK, 2, HALF]),
+                in1=sin_sb[:, ts, high].unsqueeze(2).to_broadcast([P, CHUNK, 2, HALF]),
+                op=ALU.mult,
+            )
+            nc.gpsimd.tensor_tensor(
+                out=table[:, :, :, 1, high],
+                in0=gain_sb[:, :, 1, high].unsqueeze(1).to_broadcast([P, CHUNK, 2, HALF]),
+                in1=sin_sb[:, ts, low].unsqueeze(2).to_broadcast([P, CHUNK, 2, HALF]),
+                op=ALU.mult,
+            )
+            return table
+
+        groups = [(0, PAIR), (PAIR, PAIR)] + [(c * CHUNK, CHUNK) for c in range(1, CHUNKS)]
+        group_of = {}
+        for start, count in groups:
+            for t in range(start, start + count):
+                group_of[t] = (start, count)
+        grouped_of = {}
+        codes_of = {}
+        planes_of = {}
+
+        def transpose_and_quantise(t):
+            start, count = group_of[t]
+            if t == start:
+                grouped_of[start] = front.tile(
+                    [P, count, PASSES * P * 4], BF16, name="grouped", align_bytes=64
+                )
+            x_words = x_sb[t // CHUNK][:, t % CHUNK, :].bitcast(F32)
+            flipped = psum_t.tile([P, 2 * PASSES, P], F32, name="flipped")
+            for g in range(PASSES):
+                for u in range(2):
+                    nc.tensor.transpose(
+                        flipped[:, 2 * g + u, :],
+                        x_words[:, 256 * g + u : 256 * (g + 1) : 2],
+                        ident[:],
+                    )
+            nc.scalar.copy(
+                out=grouped_of[start][:, t - start, :]
+                .bitcast(F32)
+                .rearrange("p (g m u) -> p g m u", g=PASSES, u=2),
+                in_=flipped[:].rearrange("p (g u) m -> p g m u", u=2),
+            )
+            if t == start + count - 1:
+                codes_of[start] = front.tile([P, count, PASSES * P], U32, name="codes", align_bytes=64)
+                planes_of[start] = front.tile([P, count, PASSES * P], U8, name="planes", align_bytes=64)
+                nc.vector.quantize_mx(
+                    out=codes_of[start][:].rearrange("p i c -> p (i c)").bitcast(FP8X4),
+                    scales=planes_of[start][:].rearrange("p i c -> p (i c)"),
+                    in_=grouped_of[start][:].rearrange("p i c -> p (i c)"),
+                )
+
+        def project(codes, planes):
+            banks = []
+            for n in range(N_OUT // N_PASS):
+                acc = psum_acc.tile([P, N_PASS], F32, name="acc%d" % n)
+                for g in range(PASSES):
+                    nc.tensor.matmul_mx(
+                        out=acc[:],
+                        lhsT=codes[:, g * P : (g + 1) * P].bitcast(FP8X4),
+                        lhsT_scale=planes[:, g * P : (g + 1) * P],
+                        rhs=w_words[:, g, 2 * n * N_PASS : 2 * (n + 1) * N_PASS].bitcast(FP4X4),
+                        rhs_scale=w_planes[:, g, n * N_PASS : (n + 1) * N_PASS],
+                        start=(g == 0),
+                        stop=(g == PASSES - 1),
+                    )
+                banks.append(acc)
+            return banks
+
+        def head_columns(banks, h):
+            return banks[h // Q_HEADS][:, (h % Q_HEADS) * D : (h % Q_HEADS + 1) * D]
+
+        state = {}
+        for t in range(FLIP_AHEAD):
+            transpose_and_quantise(t)
         next_table = make_tables(0)
 
         for t in range(TILES):
@@ -211,24 +214,32 @@ def tile_gemmaattention_pa_t_kernel(
                 state["prod"] = work.tile([P, PAIR * NORMED, 2, D], F32, name="prod")
                 state["qk_out"] = outs.tile([P, PAIR * NORMED, D], F32, name="qk_out")
                 state["v_out"] = outs.tile([P, PAIR, V_HEADS * D], F32, name="v_out")
-            if t + AHEAD < TILES:
-                ready[t + AHEAD] = transpose_and_quantise(t + AHEAD)
-            codes, planes = ready[t]
-            acc_kv = psum_kv.tile([P, N_PASS], F32, name="acc_kv")
-            project(codes, planes, acc_kv, 1)
-            acc_q = psum_q.tile([P, N_PASS], F32, name="acc_q")
-            project(codes, planes, acc_q, 0)
-            first = i * NORMED
-            table = state["table"]
-            nc.scalar.copy(out=state["v_out"][:, i, :], in_=acc_kv[:, K_HEADS * D : N_PASS])
-            norm_and_products(
-                acc_kv, K_HEADS, table[:, t % CHUNK, 1, :, :],
-                state["prod"][:, first + Q_HEADS : first + NORMED, :, :],
+            if t + FLIP_AHEAD < TILES:
+                transpose_and_quantise(t + FLIP_AHEAD)
+            start = group_of[t][0]
+            banks = project(codes_of[start][:, t - start, :], planes_of[start][:, t - start, :])
+
+            squares = work.tile([P, NORMED, D], BF16, name="squares")
+            sumsq = work.tile([P, NORMED], F32, name="sumsq")
+            for h in range(NORMED):
+                nc.scalar.activation(
+                    out=squares[:, h, :], in_=head_columns(banks, h), func=ACT.Square,
+                    accum_out=sumsq[:, h : h + 1],
+                )
+            rstd = work.tile([P, NORMED], F32, name="rstd")
+            nc.scalar.activation(
+                out=rstd[:], in_=sumsq[:], func=ACT.Abs_reciprocal_sqrt, scale=1.0 / D, bias=EPS
             )
-            norm_and_products(
-                acc_q, Q_HEADS, table[:, t % CHUNK, 0, :, :],
-                state["prod"][:, first : first + Q_HEADS, :, :],
-            )
+            nc.scalar.copy(out=state["v_out"][:, i, :], in_=banks[1][:, K_HEADS * D : N_PASS])
+            for h in range(NORMED):
+                nc.vector.scalar_tensor_tensor(
+                    out=state["prod"][:, i * NORMED + h, :, :],
+                    in0=head_columns(banks, h).unsqueeze(1).to_broadcast([P, 2, D]),
+                    scalar=rstd[:, h : h + 1],
+                    in1=state["table"][:, t % CHUNK, h // Q_HEADS, :, :],
+                    op0=ALU.mult,
+                    op1=ALU.mult,
+                )
             if i == PAIR - 1:
                 for half in range(2):
                     mine = slice(half * HALF, (half + 1) * HALF)

@@ -31,6 +31,7 @@ CHUNK = 4
 CHUNKS = TILES // CHUNK
 PAIR = 2
 FLIP_AHEAD = 6
+X_CHUNKS_HELD = 4
 EPS = 1e-6
 
 FLOPS = 2 * S * HID * N_OUT
@@ -49,71 +50,71 @@ def tile_gemmaattention_pa_t_kernel(
 
     with ExitStack() as ctx:
         keep = ctx.enter_context(tc.tile_pool(name="keep", bufs=1))
-        tables = ctx.enter_context(tc.tile_pool(name="tables", bufs=3))
+        tables = ctx.enter_context(tc.tile_pool(name="tables", bufs=CHUNKS))
+        xs = ctx.enter_context(tc.tile_pool(name="xs", bufs=X_CHUNKS_HELD))
         front = ctx.enter_context(tc.tile_pool(name="front", bufs=3))
         work = ctx.enter_context(tc.tile_pool(name="work", bufs=3))
         outs = ctx.enter_context(tc.tile_pool(name="outs", bufs=3))
         psum_keep = ctx.enter_context(tc.psum_pool(name="psum_keep", bufs=1))
-        psum_t = ctx.enter_context(tc.psum_pool(name="psum_t", bufs=3))
-        psum_acc = ctx.enter_context(tc.psum_pool(name="psum_acc", bufs=2))
+        psum_t = ctx.enter_context(tc.psum_pool(name="psum_t", bufs=2))
+        psum_acc = ctx.enter_context(tc.psum_pool(name="psum_acc", bufs=5))
 
-        x_sb = []
-        for c in range(CHUNKS):
-            x_sb.append(keep.tile([P, CHUNK, HID], BF16, name="x%d" % c))
+        x_sb = {}
+        for c in range(X_CHUNKS_HELD):
+            x_sb[c] = xs.tile([P, CHUNK, HID], BF16, name="x")
         w_planes = keep.tile([P, PASSES, N_OUT], U8, align_bytes=64)
         w_words = keep.tile([P, PASSES, 2 * N_OUT], U8, align_bytes=64)
         norm_w = keep.tile([P, 2, D], BF16)
         cos_sb = keep.tile([P, TILES, D], BF16)
         sin_sb = keep.tile([P, TILES, D], BF16)
 
-        nc.vector.memset(w_planes[:].bitcast(I32), 0)
-        nc.vector.memset(norm_w[:], 0.0)
+        warm_in = keep.tile([P, 1], F32)
+        warm_out = keep.tile([P, 1], F32)
+        nc.gpsimd.memset(warm_in[:], 1.0)
+        nc.scalar.activation(out=warm_out[:], in_=warm_in[:], func=ACT.Abs_reciprocal_sqrt)
 
-        nc.sync.dma_start(out=x_sb[0][:, 0:PAIR, :], in_=x_dram[:, 0:PAIR, :])
+        nc.vector.memset(norm_w[:], 0.0)
+        nc.vector.memset(w_planes[:].bitcast(I32), 0)
+
+        def load_trig(first, after):
+            nc.sync.dma_start(out=cos_sb[:, first:after, :], in_=cos_dram[:, first:after, :])
+            nc.sync.dma_start(out=sin_sb[:, first:after, :], in_=sin_dram[:, first:after, :])
+
+        nc.sync.dma_start(out=norm_w[0:1, 0, :], in_=q_norm_w.unsqueeze(0))
+        nc.sync.dma_start(out=norm_w[0:1, 1, :], in_=k_norm_w.unsqueeze(0))
+        nc.sync.dma_start(out=x_sb[0][:, 0:1, :], in_=x_dram[:, 0:1, :])
         scale_rows = w_qkv_scales.bitcast(I32).rearrange("g (q r) n -> r q g n", r=4)
         for r in range(4):
             nc.sync.dma_start(out=w_planes[r:P:32, :, :].bitcast(I32), in_=scale_rows[r])
         nc.sync.dma_start(
             out=w_words[:].bitcast(I32), in_=w_qkv_words.bitcast(I32).rearrange("g p b -> p g b")
         )
-        nc.sync.dma_start(out=norm_w[0:1, 0, :], in_=q_norm_w.unsqueeze(0))
-        nc.sync.dma_start(out=norm_w[0:1, 1, :], in_=k_norm_w.unsqueeze(0))
-        nc.sync.dma_start(out=cos_sb[:, 0:CHUNK, :], in_=cos_dram[:, 0:CHUNK, :])
-        nc.sync.dma_start(out=sin_sb[:, 0:CHUNK, :], in_=sin_dram[:, 0:CHUNK, :])
+        load_trig(0, CHUNK)
+        nc.sync.dma_start(out=x_sb[0][:, 1:PAIR, :], in_=x_dram[:, 1:PAIR, :])
+        load_trig(CHUNK, TILES // 2)
         nc.sync.dma_start(out=x_sb[0][:, PAIR:CHUNK, :], in_=x_dram[:, PAIR:CHUNK, :])
-        nc.sync.dma_start(out=cos_sb[:, CHUNK:TILES, :], in_=cos_dram[:, CHUNK:TILES, :])
-        nc.sync.dma_start(out=sin_sb[:, CHUNK:TILES, :], in_=sin_dram[:, CHUNK:TILES, :])
-        for c in range(1, CHUNKS):
+        load_trig(TILES // 2, TILES)
+        for c in range(1, X_CHUNKS_HELD):
             nc.sync.dma_start(out=x_sb[c][:], in_=x_dram[:, c * CHUNK : (c + 1) * CHUNK, :])
 
         ident = keep.tile([P, P], F32)
         make_identity(nc, ident[:])
 
-        gain_row = keep.tile([P, 2, 2, D], F32)
-        nc.vector.tensor_scalar(
-            out=gain_row[:, :, 0, :], in0=norm_w[:], scalar1=1.0, scalar2=1.0, op0=ALU.mult, op1=ALU.add
-        )
-        nc.vector.tensor_scalar(
-            out=gain_row[:, :, 1, 0:HALF], in0=norm_w[:, :, 0:HALF],
-            scalar1=1.0, scalar2=1.0, op0=ALU.mult, op1=ALU.add,
-        )
-        nc.vector.tensor_scalar(
-            out=gain_row[:, :, 1, HALF:D], in0=norm_w[:, :, HALF:D],
-            scalar1=-1.0, scalar2=-1.0, op0=ALU.mult, op1=ALU.add,
-        )
-        pick_row0 = keep.tile([P, P], F32)
-        nc.vector.memset(pick_row0[:], 0.0)
-        nc.vector.memset(pick_row0[0:1, :], 1.0)
-        gain_ps = psum_keep.tile([P, 2, 2, D], F32)
-        nc.tensor.matmul(
-            out=gain_ps[:].rearrange("p a b d -> p (a b d)"),
-            lhsT=pick_row0[:],
-            rhs=gain_row[:].rearrange("p a b d -> p (a b d)"),
-            start=True,
-            stop=True,
-        )
-        gain_sb = keep.tile([P, 2, 2, D], F32)
-        nc.scalar.copy(out=gain_sb[:], in_=gain_ps[:])
+        pick_row0 = keep.tile([P, P], BF16)
+        nc.gpsimd.memset(pick_row0[:], 0.0)
+        nc.gpsimd.memset(pick_row0[0:1, :], 1.0)
+        all_ones = keep.tile([P, 2 * D], BF16)
+        nc.gpsimd.memset(all_ones[:], 1.0)
+        gain_ps = psum_keep.tile([P, 2, D], F32)
+        gain_sb = keep.tile([P, 2, D], F32)
+
+        def spread_gains():
+            flat = gain_ps[:].rearrange("p a d -> p (a d)")
+            nc.tensor.matmul(
+                out=flat, lhsT=pick_row0[:], rhs=norm_w[:].rearrange("p a d -> p (a d)"), start=True, stop=False
+            )
+            nc.tensor.matmul(out=flat, lhsT=pick_row0[:], rhs=all_ones[:], start=False, stop=True)
+            nc.scalar.copy(out=gain_sb[:], in_=gain_ps[:])
 
         def make_tables(c):
             table = tables.tile([P, CHUNK, 2, 2, D], F32, name="table")
@@ -122,25 +123,25 @@ def tile_gemmaattention_pa_t_kernel(
             high = slice(HALF, D)
             nc.vector.tensor_tensor(
                 out=table[:, :, :, 0, :],
-                in0=gain_ps[:, :, 0, :].unsqueeze(1).to_broadcast([P, CHUNK, 2, D]),
+                in0=gain_ps[:].unsqueeze(1).to_broadcast([P, CHUNK, 2, D]),
                 in1=cos_sb[:, ts, :].unsqueeze(2).to_broadcast([P, CHUNK, 2, D]),
                 op=ALU.mult,
             )
             nc.vector.tensor_tensor(
                 out=table[:, :, :, 1, low],
-                in0=gain_ps[:, :, 1, low].unsqueeze(1).to_broadcast([P, CHUNK, 2, HALF]),
+                in0=gain_ps[:, :, low].unsqueeze(1).to_broadcast([P, CHUNK, 2, HALF]),
                 in1=sin_sb[:, ts, high].unsqueeze(2).to_broadcast([P, CHUNK, 2, HALF]),
                 op=ALU.mult,
             )
             nc.gpsimd.tensor_tensor(
                 out=table[:, :, :, 1, high],
-                in0=gain_sb[:, :, 1, high].unsqueeze(1).to_broadcast([P, CHUNK, 2, HALF]),
+                in0=gain_sb[:, :, high].unsqueeze(1).to_broadcast([P, CHUNK, 2, HALF]),
                 in1=sin_sb[:, ts, low].unsqueeze(2).to_broadcast([P, CHUNK, 2, HALF]),
                 op=ALU.mult,
             )
             return table
 
-        groups = [(0, PAIR), (PAIR, PAIR)] + [(c * CHUNK, CHUNK) for c in range(1, CHUNKS)]
+        groups = [(0, 1), (1, 1), (PAIR, PAIR)] + [(c * CHUNK, CHUNK) for c in range(1, CHUNKS)]
         group_of = {}
         for start, count in groups:
             for t in range(start, start + count):
@@ -170,6 +171,10 @@ def tile_gemmaattention_pa_t_kernel(
                 .rearrange("p (g m u) -> p g m u", g=PASSES, u=2),
                 in_=flipped[:].rearrange("p (g u) m -> p g m u", u=2),
             )
+            if t % CHUNK == CHUNK - 1 and t // CHUNK + X_CHUNKS_HELD < CHUNKS:
+                c = t // CHUNK + X_CHUNKS_HELD
+                x_sb[c] = xs.tile([P, CHUNK, HID], BF16, name="x")
+                nc.sync.dma_start(out=x_sb[c][:], in_=x_dram[:, c * CHUNK : (c + 1) * CHUNK, :])
             if t == start + count - 1:
                 codes_of[start] = front.tile([P, count, PASSES * P], U32, name="codes", align_bytes=64)
                 planes_of[start] = front.tile([P, count, PASSES * P], U8, name="planes", align_bytes=64)
@@ -182,7 +187,7 @@ def tile_gemmaattention_pa_t_kernel(
         def project(codes, planes):
             banks = []
             for n in range(N_OUT // N_PASS):
-                acc = psum_acc.tile([P, N_PASS], F32, name="acc%d" % n)
+                acc = psum_acc.tile([P, N_PASS], F32, name="acc")
                 for g in range(PASSES):
                     nc.tensor.matmul_mx(
                         out=acc[:],
@@ -199,9 +204,15 @@ def tile_gemmaattention_pa_t_kernel(
         def head_columns(banks, h):
             return banks[h // Q_HEADS][:, (h % Q_HEADS) * D : (h % Q_HEADS + 1) * D]
 
-        state = {}
-        for t in range(FLIP_AHEAD):
-            transpose_and_quantise(t)
+        state = {"flipped": 0}
+
+        def flip_up_to(count):
+            while state["flipped"] < min(count, TILES):
+                transpose_and_quantise(state["flipped"])
+                state["flipped"] += 1
+
+        spread_gains()
+        flip_up_to(PAIR)
         next_table = make_tables(0)
 
         for t in range(TILES):
@@ -214,8 +225,6 @@ def tile_gemmaattention_pa_t_kernel(
                 state["prod"] = work.tile([P, PAIR * NORMED, 2, D], F32, name="prod")
                 state["qk_out"] = outs.tile([P, PAIR * NORMED, D], F32, name="qk_out")
                 state["v_out"] = outs.tile([P, PAIR, V_HEADS * D], F32, name="v_out")
-            if t + FLIP_AHEAD < TILES:
-                transpose_and_quantise(t + FLIP_AHEAD)
             start = group_of[t][0]
             banks = project(codes_of[start][:, t - start, :], planes_of[start][:, t - start, :])
 
@@ -248,10 +257,11 @@ def tile_gemmaattention_pa_t_kernel(
                         out=state["qk_out"][:, :, mine],
                         in0=state["prod"][:, :, 0, mine],
                         in1=state["prod"][:, :, 1, other],
-                        op=ALU.add,
+                        op=(ALU.subtract if half == 0 else ALU.add),
                     )
                 ts = slice(t - PAIR + 1, t + 1)
                 by_tile = state["qk_out"][:].rearrange("p (i h) d -> p i (h d)", h=NORMED)
                 nc.sync.dma_start(out=v_dram[:, ts, :], in_=state["v_out"][:])
                 nc.sync.dma_start(out=q_dram[:, ts, :], in_=by_tile[:, :, 0 : Q_HEADS * D])
                 nc.sync.dma_start(out=k_dram[:, ts, :], in_=by_tile[:, :, Q_HEADS * D : NORMED * D])
+            flip_up_to(min(2 * t + 4, t + 1 + FLIP_AHEAD))

@@ -32,6 +32,9 @@ CHUNKS = TILES // CHUNK
 PAIR = 2
 FLIP_AHEAD = 6
 X_CHUNKS_HELD = 4
+TABLES_AHEAD = 2
+VECTOR_SINE_TILES = 1
+VECTOR_ADDS_FROM = TILES - PAIR
 EPS = 1e-6
 
 FLOPS = 2 * S * HID * N_OUT
@@ -54,6 +57,7 @@ def tile_gemmaattention_pa_t_kernel(
         xs = ctx.enter_context(tc.tile_pool(name="xs", bufs=X_CHUNKS_HELD))
         front = ctx.enter_context(tc.tile_pool(name="front", bufs=3))
         work = ctx.enter_context(tc.tile_pool(name="work", bufs=3))
+        prods = ctx.enter_context(tc.tile_pool(name="prods", bufs=6))
         outs = ctx.enter_context(tc.tile_pool(name="outs", bufs=3))
         psum_keep = ctx.enter_context(tc.psum_pool(name="psum_keep", bufs=1))
         psum_t = ctx.enter_context(tc.psum_pool(name="psum_t", bufs=2))
@@ -64,82 +68,99 @@ def tile_gemmaattention_pa_t_kernel(
             x_sb[c] = xs.tile([P, CHUNK, HID], BF16, name="x")
         w_planes = keep.tile([P, PASSES, N_OUT], U8, align_bytes=64)
         w_words = keep.tile([P, PASSES, 2 * N_OUT], U8, align_bytes=64)
-        norm_w = keep.tile([P, 2, D], BF16)
         cos_sb = keep.tile([P, TILES, D], BF16)
         sin_sb = keep.tile([P, TILES, D], BF16)
+        w_rows = keep.tile([P, 2, 2, D], BF16)
+        one_rows = keep.tile([P, 2, 2, D], BF16)
 
         warm_in = keep.tile([P, 1], F32)
         warm_out = keep.tile([P, 1], F32)
         nc.gpsimd.memset(warm_in[:], 1.0)
         nc.scalar.activation(out=warm_out[:], in_=warm_in[:], func=ACT.Abs_reciprocal_sqrt)
 
-        nc.vector.memset(norm_w[:], 0.0)
+        nc.vector.memset(w_rows[:], 0.0)
         nc.vector.memset(w_planes[:].bitcast(I32), 0)
 
         def load_trig(first, after):
             nc.sync.dma_start(out=cos_sb[:, first:after, :], in_=cos_dram[:, first:after, :])
             nc.sync.dma_start(out=sin_sb[:, first:after, :], in_=sin_dram[:, first:after, :])
 
-        nc.sync.dma_start(out=norm_w[0:1, 0, :], in_=q_norm_w.unsqueeze(0))
-        nc.sync.dma_start(out=norm_w[0:1, 1, :], in_=k_norm_w.unsqueeze(0))
-        nc.sync.dma_start(out=x_sb[0][:, 0:1, :], in_=x_dram[:, 0:1, :])
+        def load_x(c, first, after):
+            nc.sync.dma_start(
+                out=x_sb[c][:, first:after, :], in_=x_dram[:, c * CHUNK + first : c * CHUNK + after, :]
+            )
+
+        nc.sync.dma_start(out=w_rows[0:1, 0, 0, :], in_=q_norm_w.unsqueeze(0))
+        nc.sync.dma_start(out=w_rows[0:1, 0, 1, :], in_=k_norm_w.unsqueeze(0))
+        load_trig(0, CHUNK)
+        load_x(0, 0, 1)
         scale_rows = w_qkv_scales.bitcast(I32).rearrange("g (q r) n -> r q g n", r=4)
         for r in range(4):
             nc.sync.dma_start(out=w_planes[r:P:32, :, :].bitcast(I32), in_=scale_rows[r])
         nc.sync.dma_start(
             out=w_words[:].bitcast(I32), in_=w_qkv_words.bitcast(I32).rearrange("g p b -> p g b")
         )
-        load_trig(0, CHUNK)
-        nc.sync.dma_start(out=x_sb[0][:, 1:PAIR, :], in_=x_dram[:, 1:PAIR, :])
-        load_trig(CHUNK, TILES // 2)
-        nc.sync.dma_start(out=x_sb[0][:, PAIR:CHUNK, :], in_=x_dram[:, PAIR:CHUNK, :])
-        load_trig(TILES // 2, TILES)
+        load_x(0, 1, PAIR)
+        load_trig(CHUNK, 3 * CHUNK)
+        load_x(0, PAIR, CHUNK)
+        load_trig(3 * CHUNK, TILES)
         for c in range(1, X_CHUNKS_HELD):
-            nc.sync.dma_start(out=x_sb[c][:], in_=x_dram[:, c * CHUNK : (c + 1) * CHUNK, :])
-
-        ident = keep.tile([P, P], F32)
-        make_identity(nc, ident[:])
+            load_x(c, 0, CHUNK)
 
         pick_row0 = keep.tile([P, P], BF16)
         nc.gpsimd.memset(pick_row0[:], 0.0)
         nc.gpsimd.memset(pick_row0[0:1, :], 1.0)
-        all_ones = keep.tile([P, 2 * D], BF16)
-        nc.gpsimd.memset(all_ones[:], 1.0)
-        gain_ps = psum_keep.tile([P, 2, D], F32)
+        nc.gpsimd.memset(one_rows[:], 1.0)
+        nc.gpsimd.memset(one_rows[:, 1, :, 0:HALF], -1.0)
+        ident = keep.tile([P, P], F32)
+        make_identity(nc, ident[:])
+
+        nc.vector.tensor_scalar(
+            out=w_rows[:, 1, :, 0:HALF], in0=w_rows[:, 0, :, HALF:D], scalar1=-1.0, scalar2=None, op0=ALU.mult
+        )
+        nc.vector.tensor_copy(out=w_rows[:, 1, :, HALF:D], in_=w_rows[:, 0, :, 0:HALF])
+        gain_ps = psum_keep.tile([P, 2, 2, D], F32)
+        gain_flat = gain_ps[:].rearrange("p c q d -> p (c q d)")
+        nc.tensor.matmul(
+            out=gain_flat, lhsT=pick_row0[:], rhs=w_rows[:].rearrange("p c q d -> p (c q d)"),
+            start=True, stop=False,
+        )
+        nc.tensor.matmul(
+            out=gain_flat, lhsT=pick_row0[:], rhs=one_rows[:].rearrange("p c q d -> p (c q d)"),
+            start=False, stop=True,
+        )
         gain_sb = keep.tile([P, 2, D], F32)
 
-        def spread_gains():
-            flat = gain_ps[:].rearrange("p a d -> p (a d)")
-            nc.tensor.matmul(
-                out=flat, lhsT=pick_row0[:], rhs=norm_w[:].rearrange("p a d -> p (a d)"), start=True, stop=False
-            )
-            nc.tensor.matmul(out=flat, lhsT=pick_row0[:], rhs=all_ones[:], start=False, stop=True)
-            nc.scalar.copy(out=gain_sb[:], in_=gain_ps[:])
+        table_of = {}
 
         def make_tables(c):
             table = tables.tile([P, CHUNK, 2, 2, D], F32, name="table")
+            table_of[c] = table
+            slots = table[:].rearrange("p i q a (b j) -> p i q (a b) j", b=2)
             ts = slice(c * CHUNK, (c + 1) * CHUNK)
-            low = slice(0, HALF)
-            high = slice(HALF, D)
             nc.vector.tensor_tensor(
-                out=table[:, :, :, 0, :],
-                in0=gain_ps[:].unsqueeze(1).to_broadcast([P, CHUNK, 2, D]),
-                in1=cos_sb[:, ts, :].unsqueeze(2).to_broadcast([P, CHUNK, 2, D]),
+                out=slots[:, :, :, 0:4:3, :],
+                in0=gain_ps[:, 0, :, :].rearrange("p q (s j) -> p q s j", s=2)
+                .unsqueeze(1).to_broadcast([P, CHUNK, 2, 2, HALF]),
+                in1=cos_sb[:, ts, :].rearrange("p i (s j) -> p i s j", s=2)
+                .unsqueeze(2).to_broadcast([P, CHUNK, 2, 2, HALF]),
                 op=ALU.mult,
             )
+            mid = VECTOR_SINE_TILES
             nc.vector.tensor_tensor(
-                out=table[:, :, :, 1, low],
-                in0=gain_ps[:, :, low].unsqueeze(1).to_broadcast([P, CHUNK, 2, HALF]),
-                in1=sin_sb[:, ts, high].unsqueeze(2).to_broadcast([P, CHUNK, 2, HALF]),
+                out=slots[:, 0:mid, :, 1:3, :].rearrange("p i q s j -> p i q (s j)"),
+                in0=gain_ps[:, 1, :, :].unsqueeze(1).to_broadcast([P, mid, 2, D]),
+                in1=sin_sb[:, ts, :][:, 0:mid, :].unsqueeze(2).to_broadcast([P, mid, 2, D]),
                 op=ALU.mult,
             )
+            if c == 0:
+                nc.scalar.copy(out=gain_sb[:], in_=gain_ps[:, 1, :, :])
             nc.gpsimd.tensor_tensor(
-                out=table[:, :, :, 1, high],
-                in0=gain_sb[:, :, high].unsqueeze(1).to_broadcast([P, CHUNK, 2, HALF]),
-                in1=sin_sb[:, ts, low].unsqueeze(2).to_broadcast([P, CHUNK, 2, HALF]),
+                out=slots[:, mid:CHUNK, :, 1:3, :].rearrange("p i q s j -> p i q (s j)"),
+                in0=gain_sb[:].unsqueeze(1).to_broadcast([P, CHUNK - mid, 2, D]),
+                in1=sin_sb[:, ts, :][:, mid:CHUNK, :].unsqueeze(2).to_broadcast([P, CHUNK - mid, 2, D]),
                 op=ALU.mult,
             )
-            return table
 
         groups = [(0, 1), (1, 1), (PAIR, PAIR)] + [(c * CHUNK, CHUNK) for c in range(1, CHUNKS)]
         group_of = {}
@@ -174,7 +195,7 @@ def tile_gemmaattention_pa_t_kernel(
             if t % CHUNK == CHUNK - 1 and t // CHUNK + X_CHUNKS_HELD < CHUNKS:
                 c = t // CHUNK + X_CHUNKS_HELD
                 x_sb[c] = xs.tile([P, CHUNK, HID], BF16, name="x")
-                nc.sync.dma_start(out=x_sb[c][:], in_=x_dram[:, c * CHUNK : (c + 1) * CHUNK, :])
+                load_x(c, 0, CHUNK)
             if t == start + count - 1:
                 codes_of[start] = front.tile([P, count, PASSES * P], U32, name="codes", align_bytes=64)
                 planes_of[start] = front.tile([P, count, PASSES * P], U8, name="planes", align_bytes=64)
@@ -204,27 +225,38 @@ def tile_gemmaattention_pa_t_kernel(
         def head_columns(banks, h):
             return banks[h // Q_HEADS][:, (h % Q_HEADS) * D : (h % Q_HEADS + 1) * D]
 
-        state = {"flipped": 0}
+        state = {"flipped": 0, "tabled": 0}
 
         def flip_up_to(count):
             while state["flipped"] < min(count, TILES):
                 transpose_and_quantise(state["flipped"])
                 state["flipped"] += 1
 
-        spread_gains()
+        def tables_up_to(count):
+            while state["tabled"] < min(count, CHUNKS):
+                make_tables(state["tabled"])
+                state["tabled"] += 1
+
+        def add_halves(engine, prod, qk_out, i, first, after):
+            engine.tensor_tensor(
+                out=qk_out[:, i * NORMED + first : i * NORMED + after, :].rearrange("p r (a j) -> p r a j", a=2),
+                in0=prod[:, first:after, :, 0:HALF],
+                in1=prod[:, first:after, :, HALF:D],
+                op=ALU.add,
+            )
+
+        tables_up_to(1)
         flip_up_to(PAIR)
-        next_table = make_tables(0)
+        tables_up_to(1 + TABLES_AHEAD)
 
         for t in range(TILES):
             i = t % PAIR
-            if t % CHUNK == 0:
-                state["table"] = next_table
-                if t // CHUNK + 1 < CHUNKS:
-                    next_table = make_tables(t // CHUNK + 1)
             if i == 0:
-                state["prod"] = work.tile([P, PAIR * NORMED, 2, D], F32, name="prod")
                 state["qk_out"] = outs.tile([P, PAIR * NORMED, D], F32, name="qk_out")
                 state["v_out"] = outs.tile([P, PAIR, V_HEADS * D], F32, name="v_out")
+            qk_out = state["qk_out"]
+            v_out = state["v_out"]
+            by_tile = qk_out[:].rearrange("p (i h) d -> p i (h d)", h=NORMED)
             start = group_of[t][0]
             banks = project(codes_of[start][:, t - start, :], planes_of[start][:, t - start, :])
 
@@ -239,29 +271,31 @@ def tile_gemmaattention_pa_t_kernel(
             nc.scalar.activation(
                 out=rstd[:], in_=sumsq[:], func=ACT.Abs_reciprocal_sqrt, scale=1.0 / D, bias=EPS
             )
-            nc.scalar.copy(out=state["v_out"][:, i, :], in_=banks[1][:, K_HEADS * D : N_PASS])
+            nc.scalar.copy(out=v_out[:, i, :], in_=banks[1][:, K_HEADS * D : N_PASS])
+            prod = prods.tile([P, NORMED, 2, D], F32, name="prod")
             for h in range(NORMED):
                 nc.vector.scalar_tensor_tensor(
-                    out=state["prod"][:, i * NORMED + h, :, :],
+                    out=prod[:, h, :, :],
                     in0=head_columns(banks, h).unsqueeze(1).to_broadcast([P, 2, D]),
                     scalar=rstd[:, h : h + 1],
-                    in1=state["table"][:, t % CHUNK, h // Q_HEADS, :, :],
+                    in1=table_of[t // CHUNK][:, t % CHUNK, h // Q_HEADS, :, :],
                     op0=ALU.mult,
                     op1=ALU.mult,
                 )
-            if i == PAIR - 1:
-                for half in range(2):
-                    mine = slice(half * HALF, (half + 1) * HALF)
-                    other = slice((1 - half) * HALF, (2 - half) * HALF)
-                    nc.gpsimd.tensor_tensor(
-                        out=state["qk_out"][:, :, mine],
-                        in0=state["prod"][:, :, 0, mine],
-                        in1=state["prod"][:, :, 1, other],
-                        op=(ALU.subtract if half == 0 else ALU.add),
-                    )
-                ts = slice(t - PAIR + 1, t + 1)
-                by_tile = state["qk_out"][:].rearrange("p (i h) d -> p i (h d)", h=NORMED)
-                nc.sync.dma_start(out=v_dram[:, ts, :], in_=state["v_out"][:])
-                nc.sync.dma_start(out=q_dram[:, ts, :], in_=by_tile[:, :, 0 : Q_HEADS * D])
-                nc.sync.dma_start(out=k_dram[:, ts, :], in_=by_tile[:, :, Q_HEADS * D : NORMED * D])
+            if t < VECTOR_ADDS_FROM:
+                add_halves(nc.gpsimd, prod, qk_out, i, 0, NORMED)
+                if i == PAIR - 1:
+                    ts = slice(t - PAIR + 1, t + 1)
+                    nc.sync.dma_start(out=v_dram[:, ts, :], in_=v_out[:])
+                    nc.sync.dma_start(out=q_dram[:, ts, :], in_=by_tile[:, :, 0 : Q_HEADS * D])
+                    nc.sync.dma_start(out=k_dram[:, ts, :], in_=by_tile[:, :, Q_HEADS * D : NORMED * D])
+            else:
+                ts = slice(t, t + 1)
+                nc.sync.dma_start(out=v_dram[:, ts, :], in_=v_out[:, i : i + 1, :])
+                add_halves(nc.vector, prod, qk_out, i, 0, Q_HEADS)
+                nc.sync.dma_start(out=q_dram[:, ts, :], in_=by_tile[:, i : i + 1, 0 : Q_HEADS * D])
+                add_halves(nc.vector, prod, qk_out, i, Q_HEADS, NORMED)
+                nc.sync.dma_start(out=k_dram[:, ts, :], in_=by_tile[:, i : i + 1, Q_HEADS * D : NORMED * D])
             flip_up_to(min(2 * t + 4, t + 1 + FLIP_AHEAD))
+            if t % CHUNK == 0:
+                tables_up_to(t // CHUNK + 2 + TABLES_AHEAD)

@@ -33,8 +33,8 @@ PAIR = 2
 FLIP_AHEAD = 6
 X_CHUNKS_HELD = 4
 TABLES_AHEAD = 2
-VECTOR_SINE_TILES = 1
-VECTOR_ADDS_FROM = TILES - PAIR
+VECTOR_SINE_TILES = 2
+VECTOR_ADDS_FROM = TILES - 1
 EPS = 1e-6
 
 FLOPS = 2 * S * HID * N_OUT
@@ -121,44 +121,57 @@ def tile_gemmaattention_pa_t_kernel(
         nc.vector.tensor_copy(out=w_rows[:, 1, :, HALF:D], in_=w_rows[:, 0, :, 0:HALF])
         gain_ps = psum_keep.tile([P, 2, 2, D], F32)
         gain_flat = gain_ps[:].rearrange("p c q d -> p (c q d)")
+        gain_too = psum_t.tile([P, 2 * PASSES, P], F32, name="flipped")
+        too_flat = gain_too[:].rearrange("p c d -> p (c d)")[:, 0 : 2 * D]
         nc.tensor.matmul(
-            out=gain_flat, lhsT=pick_row0[:], rhs=w_rows[:].rearrange("p c q d -> p (c q d)"),
+            out=gain_flat, lhsT=pick_row0[:], rhs=one_rows[:].rearrange("p c q d -> p (c q d)"),
             start=True, stop=False,
         )
         nc.tensor.matmul(
-            out=gain_flat, lhsT=pick_row0[:], rhs=one_rows[:].rearrange("p c q d -> p (c q d)"),
+            out=too_flat, lhsT=pick_row0[:], rhs=one_rows[:, 1, :, :].rearrange("p q d -> p (q d)"),
+            start=True, stop=False,
+        )
+        nc.tensor.matmul(
+            out=gain_flat, lhsT=pick_row0[:], rhs=w_rows[:].rearrange("p c q d -> p (c q d)"),
+            start=False, stop=True,
+        )
+        nc.tensor.matmul(
+            out=too_flat, lhsT=pick_row0[:], rhs=w_rows[:, 1, :, :].rearrange("p q d -> p (q d)"),
             start=False, stop=True,
         )
         gain_sb = keep.tile([P, 2, D], F32)
+        nc.scalar.copy(out=gain_sb[:].rearrange("p q d -> p (q d)"), in_=too_flat)
 
         table_of = {}
 
+        mid = VECTOR_SINE_TILES
+
+        def slots_of(c):
+            return table_of[c][:].rearrange("p i q a (b j) -> p i q (a b) j", b=2)
+
         def make_tables(c):
-            table = tables.tile([P, CHUNK, 2, 2, D], F32, name="table")
-            table_of[c] = table
-            slots = table[:].rearrange("p i q a (b j) -> p i q (a b) j", b=2)
             ts = slice(c * CHUNK, (c + 1) * CHUNK)
             nc.vector.tensor_tensor(
-                out=slots[:, :, :, 0:4:3, :],
+                out=slots_of(c)[:, :, :, 0:4:3, :],
                 in0=gain_ps[:, 0, :, :].rearrange("p q (s j) -> p q s j", s=2)
                 .unsqueeze(1).to_broadcast([P, CHUNK, 2, 2, HALF]),
                 in1=cos_sb[:, ts, :].rearrange("p i (s j) -> p i s j", s=2)
                 .unsqueeze(2).to_broadcast([P, CHUNK, 2, 2, HALF]),
                 op=ALU.mult,
             )
-            mid = VECTOR_SINE_TILES
             nc.vector.tensor_tensor(
-                out=slots[:, 0:mid, :, 1:3, :].rearrange("p i q s j -> p i q (s j)"),
+                out=slots_of(c)[:, 0:mid, :, 1:3, :].rearrange("p i q s j -> p i q (s j)"),
                 in0=gain_ps[:, 1, :, :].unsqueeze(1).to_broadcast([P, mid, 2, D]),
-                in1=sin_sb[:, ts, :][:, 0:mid, :].unsqueeze(2).to_broadcast([P, mid, 2, D]),
+                in1=sin_sb[:, c * CHUNK : c * CHUNK + mid, :].unsqueeze(2).to_broadcast([P, mid, 2, D]),
                 op=ALU.mult,
             )
-            if c == 0:
-                nc.scalar.copy(out=gain_sb[:], in_=gain_ps[:, 1, :, :])
+
+        def make_tables_on_gpsimd(c):
             nc.gpsimd.tensor_tensor(
-                out=slots[:, mid:CHUNK, :, 1:3, :].rearrange("p i q s j -> p i q (s j)"),
+                out=slots_of(c)[:, mid:CHUNK, :, 1:3, :].rearrange("p i q s j -> p i q (s j)"),
                 in0=gain_sb[:].unsqueeze(1).to_broadcast([P, CHUNK - mid, 2, D]),
-                in1=sin_sb[:, ts, :][:, mid:CHUNK, :].unsqueeze(2).to_broadcast([P, CHUNK - mid, 2, D]),
+                in1=sin_sb[:, c * CHUNK + mid : (c + 1) * CHUNK, :]
+                .unsqueeze(2).to_broadcast([P, CHUNK - mid, 2, D]),
                 op=ALU.mult,
             )
 
@@ -245,7 +258,11 @@ def tile_gemmaattention_pa_t_kernel(
                 op=ALU.add,
             )
 
+        for c in range(CHUNKS):
+            table_of[c] = tables.tile([P, CHUNK, 2, 2, D], F32, name="table")
         tables_up_to(1)
+        for c in range(CHUNKS):
+            make_tables_on_gpsimd(c)
         flip_up_to(PAIR)
         tables_up_to(1 + TABLES_AHEAD)
 
@@ -282,8 +299,9 @@ def tile_gemmaattention_pa_t_kernel(
                     op0=ALU.mult,
                     op1=ALU.mult,
                 )
-            if t < VECTOR_ADDS_FROM:
-                add_halves(nc.gpsimd, prod, qk_out, i, 0, NORMED)
+            adder = nc.vector if t >= VECTOR_ADDS_FROM else nc.gpsimd
+            if t < TILES - PAIR:
+                add_halves(adder, prod, qk_out, i, 0, NORMED)
                 if i == PAIR - 1:
                     ts = slice(t - PAIR + 1, t + 1)
                     nc.sync.dma_start(out=v_dram[:, ts, :], in_=v_out[:])
@@ -292,9 +310,9 @@ def tile_gemmaattention_pa_t_kernel(
             else:
                 ts = slice(t, t + 1)
                 nc.sync.dma_start(out=v_dram[:, ts, :], in_=v_out[:, i : i + 1, :])
-                add_halves(nc.vector, prod, qk_out, i, 0, Q_HEADS)
+                add_halves(adder, prod, qk_out, i, 0, Q_HEADS)
                 nc.sync.dma_start(out=q_dram[:, ts, :], in_=by_tile[:, i : i + 1, 0 : Q_HEADS * D])
-                add_halves(nc.vector, prod, qk_out, i, Q_HEADS, NORMED)
+                add_halves(adder, prod, qk_out, i, Q_HEADS, NORMED)
                 nc.sync.dma_start(out=k_dram[:, ts, :], in_=by_tile[:, i : i + 1, Q_HEADS * D : NORMED * D])
             flip_up_to(min(2 * t + 4, t + 1 + FLIP_AHEAD))
             if t % CHUNK == 0:

@@ -12,6 +12,7 @@ FP8X4 = mybir.dt.float8_e4m3fn_x4
 FP4X4 = mybir.dt.float4_e2m1fn_x4
 ALU = mybir.AluOpType
 ACT = mybir.ActivationFunctionType
+EngineType = mybir.EngineType
 
 P = 128
 S = 4096
@@ -34,7 +35,10 @@ FLIP_AHEAD = 6
 X_CHUNKS_HELD = 4
 TABLES_AHEAD = 2
 VECTOR_SINE_TILES = 2
+TENSOR_CHUNKS = (5, 6, 7)
+TENSOR_STEPS = (5, 7, 8, 10, 11, 13, 14, 16, 17, 19, 20, 22, 23, 25, 26)
 VECTOR_ADDS_FROM = TILES - 1
+ONES_ROW = 64
 EPS = 1e-6
 
 FLOPS = 2 * S * HID * N_OUT
@@ -70,17 +74,14 @@ def tile_gemmaattention_pa_t_kernel(
         w_words = keep.tile([P, PASSES, 2 * N_OUT], U8, align_bytes=64)
         cos_sb = keep.tile([P, TILES, D], BF16)
         sin_sb = keep.tile([P, TILES, D], BF16)
-        w_rows = keep.tile([P, 2, 2, D], BF16)
-        one_rows = keep.tile([P, 2, 2, D], BF16)
+        w_rows = keep.tile([P, 2, D], BF16)
+        signs = keep.tile([P, 2, 2, D], BF16)
+        diag_ones = keep.tile([P, 2, 2, D], BF16)
+        diag_w = keep.tile([P, 2, 2, D], BF16)
+        turned = ctx.enter_context(tc.tile_pool(name="turned", bufs=2))
 
         warm_in = keep.tile([P, 1], F32)
         warm_out = keep.tile([P, 1], F32)
-        nc.gpsimd.memset(warm_in[:], 1.0)
-        nc.scalar.activation(out=warm_out[:], in_=warm_in[:], func=ACT.Abs_reciprocal_sqrt)
-
-        nc.vector.memset(w_rows[:], 0.0)
-        nc.vector.memset(w_planes[:].bitcast(I32), 0)
-
         def load_trig(first, after):
             nc.sync.dma_start(out=cos_sb[:, first:after, :], in_=cos_dram[:, first:after, :])
             nc.sync.dma_start(out=sin_sb[:, first:after, :], in_=sin_dram[:, first:after, :])
@@ -90,57 +91,22 @@ def tile_gemmaattention_pa_t_kernel(
                 out=x_sb[c][:, first:after, :], in_=x_dram[:, c * CHUNK + first : c * CHUNK + after, :]
             )
 
-        nc.sync.dma_start(out=w_rows[0:1, 0, 0, :], in_=q_norm_w.unsqueeze(0))
-        nc.sync.dma_start(out=w_rows[0:1, 0, 1, :], in_=k_norm_w.unsqueeze(0))
-        load_trig(0, CHUNK)
-        load_x(0, 0, 1)
-        scale_rows = w_qkv_scales.bitcast(I32).rearrange("g (q r) n -> r q g n", r=4)
-        for r in range(4):
-            nc.sync.dma_start(out=w_planes[r:P:32, :, :].bitcast(I32), in_=scale_rows[r])
-        nc.sync.dma_start(
-            out=w_words[:].bitcast(I32), in_=w_qkv_words.bitcast(I32).rearrange("g p b -> p g b")
-        )
-        load_x(0, 1, PAIR)
-        load_trig(CHUNK, 3 * CHUNK)
-        load_x(0, PAIR, CHUNK)
-        load_trig(3 * CHUNK, TILES)
-        for c in range(1, X_CHUNKS_HELD):
-            load_x(c, 0, CHUNK)
-
-        pick_row0 = keep.tile([P, P], BF16)
-        nc.gpsimd.memset(pick_row0[:], 0.0)
-        nc.gpsimd.memset(pick_row0[0:1, :], 1.0)
-        nc.gpsimd.memset(one_rows[:], 1.0)
-        nc.gpsimd.memset(one_rows[:, 1, :, 0:HALF], -1.0)
+        pick = keep.tile([P, P], BF16)
+        pick_minus = keep.tile([P, P], BF16)
+        for tile, value in ((pick, 1.0), (pick_minus, -1.0)):
+            nc.gpsimd.memset(tile[:], 0.0)
+            nc.gpsimd.memset(tile[0:1, :], value)
+            nc.gpsimd.memset(tile[ONES_ROW : ONES_ROW + 1, :], value)
         ident = keep.tile([P, P], F32)
         make_identity(nc, ident[:])
-
-        nc.vector.tensor_scalar(
-            out=w_rows[:, 1, :, 0:HALF], in0=w_rows[:, 0, :, HALF:D], scalar1=-1.0, scalar2=None, op0=ALU.mult
+        nc.gpsimd.memset(signs[:], 1.0)
+        nc.gpsimd.memset(signs[:, 1, :, 0:HALF], -1.0)
+        nc.gpsimd.tensor_tensor(
+            out=diag_ones[:].rearrange("p c q d -> p (c q) d"),
+            in0=signs[:].rearrange("p c q d -> p (c q) d"),
+            in1=ident[:].unsqueeze(1).to_broadcast([P, 4, D]),
+            op=ALU.mult,
         )
-        nc.vector.tensor_copy(out=w_rows[:, 1, :, HALF:D], in_=w_rows[:, 0, :, 0:HALF])
-        gain_ps = psum_keep.tile([P, 2, 2, D], F32)
-        gain_flat = gain_ps[:].rearrange("p c q d -> p (c q d)")
-        gain_too = psum_t.tile([P, 2 * PASSES, P], F32, name="flipped")
-        too_flat = gain_too[:].rearrange("p c d -> p (c d)")[:, 0 : 2 * D]
-        nc.tensor.matmul(
-            out=gain_flat, lhsT=pick_row0[:], rhs=one_rows[:].rearrange("p c q d -> p (c q d)"),
-            start=True, stop=False,
-        )
-        nc.tensor.matmul(
-            out=too_flat, lhsT=pick_row0[:], rhs=one_rows[:, 1, :, :].rearrange("p q d -> p (q d)"),
-            start=True, stop=False,
-        )
-        nc.tensor.matmul(
-            out=gain_flat, lhsT=pick_row0[:], rhs=w_rows[:].rearrange("p c q d -> p (c q d)"),
-            start=False, stop=True,
-        )
-        nc.tensor.matmul(
-            out=too_flat, lhsT=pick_row0[:], rhs=w_rows[:, 1, :, :].rearrange("p q d -> p (q d)"),
-            start=False, stop=True,
-        )
-        gain_sb = keep.tile([P, 2, D], F32)
-        nc.scalar.copy(out=gain_sb[:].rearrange("p q d -> p (q d)"), in_=too_flat)
 
         table_of = {}
 
@@ -175,6 +141,49 @@ def tile_gemmaattention_pa_t_kernel(
                 op=ALU.mult,
             )
 
+        def make_diag_w():
+            for c, first, after, one in ((0, 0, D, -1.0), (1, 0, HALF, 1.0), (1, HALF, D, -1.0)):
+                nc.vector.scalar_tensor_tensor(
+                    out=diag_w[:, c, :, first:after],
+                    in0=gain_ps[:, c, :, first:after],
+                    scalar=one,
+                    in1=ident[:, first:after].unsqueeze(1).to_broadcast([P, 2, after - first]),
+                    op0=ALU.add,
+                    op1=ALU.mult,
+                )
+
+        turned_of = {}
+
+        def turn_trig(c):
+            aux = psum_keep.tile([P, 2 * CHUNK, P], BF16, name="aux")
+            for i in range(CHUNK):
+                nc.tensor.transpose(aux[:, i, :], cos_sb[:, c * CHUNK + i, :], diag_ones[:, 0, 0, :])
+                nc.tensor.transpose(aux[:, CHUNK + i, :], sin_sb[:, c * CHUNK + i, :], diag_ones[:, 0, 0, :])
+            turned_of[c] = turned.tile([P, 2 * CHUNK, P], BF16, name="trig")
+            nc.scalar.copy(out=turned_of[c][:], in_=aux[:])
+
+        def make_table_on_tensor(c, i):
+            aux = psum_keep.tile([P, 2, 4, HALF], F32, name="aux")
+            for f, slots in ((0, slice(0, 4, 3)), (1, slice(1, 3))):
+                for rhs, first in ((diag_ones, True), (diag_w, False)):
+                    nc.tensor.matmul(
+                        out=aux[:, :, slots, :],
+                        lhsT=turned_of[c][:, CHUNK * f + i, :],
+                        rhs=rhs[:, f, :, :].rearrange("p q (s j) -> p q s j", s=2),
+                        start=first, stop=not first,
+                    )
+            nc.scalar.copy(
+                out=table_of[c][:, i, :, :, :].rearrange("p q a d -> p (q a d)"),
+                in_=aux[:].rearrange("p q s j -> p (q s j)"),
+            )
+
+        def tensor_piece(n):
+            c = TENSOR_CHUNKS[n // (1 + CHUNK)]
+            if n % (1 + CHUNK) == 0:
+                turn_trig(c)
+            else:
+                make_table_on_tensor(c, n % (1 + CHUNK) - 1)
+
         groups = [(0, 1), (1, 1), (PAIR, PAIR)] + [(c * CHUNK, CHUNK) for c in range(1, CHUNKS)]
         group_of = {}
         for start, count in groups:
@@ -184,7 +193,7 @@ def tile_gemmaattention_pa_t_kernel(
         codes_of = {}
         planes_of = {}
 
-        def transpose_and_quantise(t):
+        def flip(t):
             start, count = group_of[t]
             if t == start:
                 grouped_of[start] = front.tile(
@@ -209,6 +218,9 @@ def tile_gemmaattention_pa_t_kernel(
                 c = t // CHUNK + X_CHUNKS_HELD
                 x_sb[c] = xs.tile([P, CHUNK, HID], BF16, name="x")
                 load_x(c, 0, CHUNK)
+
+        def quantise(t):
+            start, count = group_of[t]
             if t == start + count - 1:
                 codes_of[start] = front.tile([P, count, PASSES * P], U32, name="codes", align_bytes=64)
                 planes_of[start] = front.tile([P, count, PASSES * P], U8, name="planes", align_bytes=64)
@@ -218,7 +230,12 @@ def tile_gemmaattention_pa_t_kernel(
                     in_=grouped_of[start][:].rearrange("p i c -> p (i c)"),
                 )
 
-        def project(codes, planes):
+        banks_of = {}
+
+        def multiply(t):
+            start = group_of[t][0]
+            codes = codes_of[start][:, t - start, :]
+            planes = planes_of[start][:, t - start, :]
             banks = []
             for n in range(N_OUT // N_PASS):
                 acc = psum_acc.tile([P, N_PASS], F32, name="acc")
@@ -233,22 +250,10 @@ def tile_gemmaattention_pa_t_kernel(
                         stop=(g == PASSES - 1),
                     )
                 banks.append(acc)
-            return banks
+            banks_of[t] = banks
 
         def head_columns(banks, h):
             return banks[h // Q_HEADS][:, (h % Q_HEADS) * D : (h % Q_HEADS + 1) * D]
-
-        state = {"flipped": 0, "tabled": 0}
-
-        def flip_up_to(count):
-            while state["flipped"] < min(count, TILES):
-                transpose_and_quantise(state["flipped"])
-                state["flipped"] += 1
-
-        def tables_up_to(count):
-            while state["tabled"] < min(count, CHUNKS):
-                make_tables(state["tabled"])
-                state["tabled"] += 1
 
         def add_halves(engine, prod, qk_out, i, first, after):
             engine.tensor_tensor(
@@ -260,23 +265,17 @@ def tile_gemmaattention_pa_t_kernel(
 
         for c in range(CHUNKS):
             table_of[c] = tables.tile([P, CHUNK, 2, 2, D], F32, name="table")
-        tables_up_to(1)
-        for c in range(CHUNKS):
-            make_tables_on_gpsimd(c)
-        flip_up_to(PAIR)
-        tables_up_to(1 + TABLES_AHEAD)
+        outs_of = {}
+        rstd_of = {}
 
-        for t in range(TILES):
+        def normalise(t):
+            banks = banks_of[t]
             i = t % PAIR
             if i == 0:
-                state["qk_out"] = outs.tile([P, PAIR * NORMED, D], F32, name="qk_out")
-                state["v_out"] = outs.tile([P, PAIR, V_HEADS * D], F32, name="v_out")
-            qk_out = state["qk_out"]
-            v_out = state["v_out"]
-            by_tile = qk_out[:].rearrange("p (i h) d -> p i (h d)", h=NORMED)
-            start = group_of[t][0]
-            banks = project(codes_of[start][:, t - start, :], planes_of[start][:, t - start, :])
-
+                qk_out = outs.tile([P, PAIR * NORMED, D], F32, name="qk_out")
+                v_out = outs.tile([P, PAIR, V_HEADS * D], F32, name="v_out")
+                outs_of[t] = (qk_out, v_out)
+            v_out = outs_of[t - i][1]
             squares = work.tile([P, NORMED, D], BF16, name="squares")
             sumsq = work.tile([P, NORMED], F32, name="sumsq")
             for h in range(NORMED):
@@ -288,9 +287,19 @@ def tile_gemmaattention_pa_t_kernel(
             nc.scalar.activation(
                 out=rstd[:], in_=sumsq[:], func=ACT.Abs_reciprocal_sqrt, scale=1.0 / D, bias=EPS
             )
+            rstd_of[t] = rstd
             nc.scalar.copy(out=v_out[:, i, :], in_=banks[1][:, K_HEADS * D : N_PASS])
+
+        def rotate(t, between=None):
+            banks = banks_of[t]
+            rstd = rstd_of[t]
+            i = t % PAIR
+            qk_out, v_out = outs_of[t - i]
+            by_tile = qk_out[:].rearrange("p (i h) d -> p i (h d)", h=NORMED)
             prod = prods.tile([P, NORMED, 2, D], F32, name="prod")
             for h in range(NORMED):
+                if between is not None and h == NORMED // 2:
+                    between()
                 nc.vector.scalar_tensor_tensor(
                     out=prod[:, h, :, :],
                     in0=head_columns(banks, h).unsqueeze(1).to_broadcast([P, 2, D]),
@@ -314,6 +323,72 @@ def tile_gemmaattention_pa_t_kernel(
                 nc.sync.dma_start(out=q_dram[:, ts, :], in_=by_tile[:, i : i + 1, 0 : Q_HEADS * D])
                 add_halves(adder, prod, qk_out, i, Q_HEADS, NORMED)
                 nc.sync.dma_start(out=k_dram[:, ts, :], in_=by_tile[:, i : i + 1, Q_HEADS * D : NORMED * D])
-            flip_up_to(min(2 * t + 4, t + 1 + FLIP_AHEAD))
-            if t % CHUNK == 0:
-                tables_up_to(t // CHUNK + 2 + TABLES_AHEAD)
+
+        with tc.manual_schedule(engines={EngineType.SP, EngineType.PE, EngineType.Activation, EngineType.DVE}):
+            nc.gpsimd.memset(warm_in[:], 1.0)
+            nc.vector.memset(w_rows[:], 0.0)
+            nc.vector.memset(w_rows[ONES_ROW : ONES_ROW + 1, :, :], 1.0)
+            nc.scalar.dma_start(out=w_rows[0:1, 1, :], in_=k_norm_w.unsqueeze(0))
+            nc.scalar.activation(out=warm_out[:], in_=warm_in[:], func=ACT.Abs_reciprocal_sqrt)
+            nc.vector.memset(w_planes[:].bitcast(I32), 0)
+            load_x(0, 0, 1)
+            nc.sync.dma_start(out=w_rows[0:1, 0, :], in_=q_norm_w.unsqueeze(0))
+            nc.sync.dma_start(
+                out=w_words[:].bitcast(I32), in_=w_qkv_words.bitcast(I32).rearrange("g p b -> p g b")
+            )
+            scale_rows = w_qkv_scales.bitcast(I32).rearrange("g (q r) n -> r q g n", r=4)
+            for r in range(4):
+                nc.sync.dma_start(out=w_planes[r:P:32, :, :].bitcast(I32), in_=scale_rows[r])
+            load_trig(0, CHUNK)
+            load_x(0, 1, PAIR)
+            load_trig(CHUNK, 3 * CHUNK)
+            load_x(0, PAIR, CHUNK)
+            load_x(1, 0, CHUNK)
+            load_trig(3 * CHUNK, TILES)
+            for c in range(2, X_CHUNKS_HELD):
+                load_x(c, 0, CHUNK)
+            flip(0)
+            quantise(0)
+            gain_ps = psum_keep.tile([P, 2, 2, D], F32, name="aux")
+            gain_too = psum_t.tile([P, 2 * PASSES, P], F32, name="flipped")
+            nc.tensor.matmul(out=gain_ps[:, 0, :, :], lhsT=pick[:], rhs=w_rows[:], start=True, stop=True)
+            for gain_1 in (gain_ps[:, 1, :, :], gain_too[:, 0:2, :]):
+                nc.tensor.matmul(
+                    out=gain_1[:, :, 0:HALF], lhsT=pick_minus[:], rhs=w_rows[:, :, HALF:D], start=True, stop=True
+                )
+                nc.tensor.matmul(
+                    out=gain_1[:, :, HALF:D], lhsT=pick[:], rhs=w_rows[:, :, 0:HALF], start=True, stop=True
+                )
+            gain_sb = keep.tile([P, 2, D], F32)
+            nc.scalar.copy(out=gain_sb[:], in_=gain_too[:, 0:2, :])
+            make_tables(0)
+            make_tables_on_gpsimd(0)
+            multiply(0)
+            make_diag_w()
+            normalise(0)
+            flip(1)
+            rotate(0, between=lambda: quantise(1))
+            make_tables_on_gpsimd(1)
+            flip(2)
+            flip(3)
+            multiply(1)
+            quantise(3)
+            make_tables(1)
+            normalise(1)
+            rotate(1)
+        flips = PAIR * 2
+        tables_made = 2
+        for t in range(2, TILES):
+            multiply(t)
+            normalise(t)
+            rotate(t)
+            while flips < min(2 * t + 4, t + 1 + FLIP_AHEAD, TILES):
+                flip(flips)
+                quantise(flips)
+                flips += 1
+            if tables_made not in TENSOR_CHUNKS and tables_made < CHUNKS:
+                make_tables(tables_made)
+                make_tables_on_gpsimd(tables_made)
+                tables_made += 1
+            if t in TENSOR_STEPS:
+                tensor_piece(TENSOR_STEPS.index(t))

@@ -31,9 +31,9 @@ TILES = S // P
 CHUNK = 4
 CHUNKS = TILES // CHUNK
 PAIR = 2
-FLIP_AHEAD = 6
+FLIP_AHEAD = 7
 X_CHUNKS_HELD = 4
-TABLES_AHEAD = 2
+VECTOR_PIECES = 3
 VECTOR_SINE_TILES = 2
 TENSOR_CHUNKS = (5, 6, 7)
 TENSOR_STEPS = (5, 7, 8, 10, 11, 13, 14, 16, 17, 19, 20, 22, 23, 25, 26)
@@ -115,22 +115,29 @@ def tile_gemmaattention_pa_t_kernel(
         def slots_of(c):
             return table_of[c][:].rearrange("p i q a (b j) -> p i q (a b) j", b=2)
 
+        def vector_table(c, piece):
+            first = 0 if piece < 2 else mid
+            ts = slice(c * CHUNK + first, c * CHUNK + first + mid)
+            if piece == 1:
+                nc.vector.tensor_tensor(
+                    out=slots_of(c)[:, 0:mid, :, 1:3, :].rearrange("p i q s j -> p i q (s j)"),
+                    in0=gain_ps[:, 1, :, :].unsqueeze(1).to_broadcast([P, mid, 2, D]),
+                    in1=sin_sb[:, ts, :].unsqueeze(2).to_broadcast([P, mid, 2, D]),
+                    op=ALU.mult,
+                )
+            else:
+                nc.vector.tensor_tensor(
+                    out=slots_of(c)[:, first : first + mid, :, 0:4:3, :],
+                    in0=gain_ps[:, 0, :, :].rearrange("p q (s j) -> p q s j", s=2)
+                    .unsqueeze(1).to_broadcast([P, mid, 2, 2, HALF]),
+                    in1=cos_sb[:, ts, :].rearrange("p i (s j) -> p i s j", s=2)
+                    .unsqueeze(2).to_broadcast([P, mid, 2, 2, HALF]),
+                    op=ALU.mult,
+                )
+
         def make_tables(c):
-            ts = slice(c * CHUNK, (c + 1) * CHUNK)
-            nc.vector.tensor_tensor(
-                out=slots_of(c)[:, :, :, 0:4:3, :],
-                in0=gain_ps[:, 0, :, :].rearrange("p q (s j) -> p q s j", s=2)
-                .unsqueeze(1).to_broadcast([P, CHUNK, 2, 2, HALF]),
-                in1=cos_sb[:, ts, :].rearrange("p i (s j) -> p i s j", s=2)
-                .unsqueeze(2).to_broadcast([P, CHUNK, 2, 2, HALF]),
-                op=ALU.mult,
-            )
-            nc.vector.tensor_tensor(
-                out=slots_of(c)[:, 0:mid, :, 1:3, :].rearrange("p i q s j -> p i q (s j)"),
-                in0=gain_ps[:, 1, :, :].unsqueeze(1).to_broadcast([P, mid, 2, D]),
-                in1=sin_sb[:, c * CHUNK : c * CHUNK + mid, :].unsqueeze(2).to_broadcast([P, mid, 2, D]),
-                op=ALU.mult,
-            )
+            for piece in range(VECTOR_PIECES):
+                vector_table(c, piece)
 
         def make_tables_on_gpsimd(c):
             nc.gpsimd.tensor_tensor(
@@ -155,7 +162,7 @@ def tile_gemmaattention_pa_t_kernel(
         turned_of = {}
 
         def turn_trig(c):
-            aux = psum_keep.tile([P, 2 * CHUNK, P], BF16, name="aux")
+            aux = psum_t.tile([P, 2 * CHUNK, P], BF16, name="flipped")
             for i in range(CHUNK):
                 nc.tensor.transpose(aux[:, i, :], cos_sb[:, c * CHUNK + i, :], diag_ones[:, 0, 0, :])
                 nc.tensor.transpose(aux[:, CHUNK + i, :], sin_sb[:, c * CHUNK + i, :], diag_ones[:, 0, 0, :])
@@ -163,7 +170,7 @@ def tile_gemmaattention_pa_t_kernel(
             nc.scalar.copy(out=turned_of[c][:], in_=aux[:])
 
         def make_table_on_tensor(c, i):
-            aux = psum_keep.tile([P, 2, 4, HALF], F32, name="aux")
+            aux = psum_t.tile([P, 2, 4, HALF], F32, name="flipped")
             for f, slots in ((0, slice(0, 4, 3)), (1, slice(1, 3))):
                 for rhs, first in ((diag_ones, True), (diag_w, False)):
                     nc.tensor.matmul(
@@ -184,7 +191,7 @@ def tile_gemmaattention_pa_t_kernel(
             else:
                 make_table_on_tensor(c, n % (1 + CHUNK) - 1)
 
-        groups = [(0, 1), (1, 1), (PAIR, PAIR)] + [(c * CHUNK, CHUNK) for c in range(1, CHUNKS)]
+        groups = [(0, 1), (1, 1), (2, PAIR), (4, PAIR), (6, PAIR)] + [(c * CHUNK, CHUNK) for c in range(2, CHUNKS)]
         group_of = {}
         for start, count in groups:
             for t in range(start, start + count):
@@ -290,7 +297,7 @@ def tile_gemmaattention_pa_t_kernel(
             rstd_of[t] = rstd
             nc.scalar.copy(out=v_out[:, i, :], in_=banks[1][:, K_HEADS * D : N_PASS])
 
-        def rotate(t, between=None):
+        def rotate(t, between=None, between_at=NORMED // 2):
             banks = banks_of[t]
             rstd = rstd_of[t]
             i = t % PAIR
@@ -298,7 +305,7 @@ def tile_gemmaattention_pa_t_kernel(
             by_tile = qk_out[:].rearrange("p (i h) d -> p i (h d)", h=NORMED)
             prod = prods.tile([P, NORMED, 2, D], F32, name="prod")
             for h in range(NORMED):
-                if between is not None and h == NORMED // 2:
+                if between is not None and h == between_at:
                     between()
                 nc.vector.scalar_tensor_tensor(
                     out=prod[:, h, :, :],
@@ -376,19 +383,31 @@ def tile_gemmaattention_pa_t_kernel(
             make_tables(1)
             normalise(1)
             rotate(1)
-        flips = PAIR * 2
-        tables_made = 2
-        for t in range(2, TILES):
-            multiply(t)
-            normalise(t)
-            rotate(t)
-            while flips < min(2 * t + 4, t + 1 + FLIP_AHEAD, TILES):
-                flip(flips)
-                quantise(flips)
-                flips += 1
-            if tables_made not in TENSOR_CHUNKS and tables_made < CHUNKS:
-                make_tables(tables_made)
-                make_tables_on_gpsimd(tables_made)
-                tables_made += 1
-            if t in TENSOR_STEPS:
-                tensor_piece(TENSOR_STEPS.index(t))
+            flip(4)
+            flip(5)
+        quantise_after = {2: 4, 3: 6}
+        for c in range(2, CHUNKS):
+            quantise_after[c * CHUNK - 3] = c * CHUNK
+        table_work = [(c, piece) for c in range(2, CHUNKS) if c not in TENSOR_CHUNKS for piece in range(VECTOR_PIECES)]
+        flips = 6
+        tables_done = 0
+        with tc.manual_schedule(engines={EngineType.DVE}):
+            for t in range(2, TILES):
+                multiply(t)
+                normalise(t)
+                if tables_done < len(table_work) and t not in quantise_after:
+                    c, piece = table_work[tables_done]
+                    tables_done += 1
+                    if piece == 0:
+                        make_tables_on_gpsimd(c)
+                    rotate(t, between=lambda: vector_table(c, piece), between_at=NORMED - 1)
+                else:
+                    rotate(t)
+                if t in quantise_after:
+                    start = quantise_after[t]
+                    quantise(start + group_of[start][1] - 1)
+                while flips < min(2 * t + 4, t + 1 + FLIP_AHEAD, TILES):
+                    flip(flips)
+                    flips += 1
+                if t in TENSOR_STEPS:
+                    tensor_piece(TENSOR_STEPS.index(t))

@@ -35,8 +35,8 @@ FLIP_AHEAD = 7
 X_CHUNKS_HELD = 4
 VECTOR_PIECES = 3
 VECTOR_SINE_TILES = 2
-TENSOR_CHUNKS = (5, 6, 7)
-TENSOR_STEPS = (5, 7, 8, 10, 11, 13, 14, 16, 17, 19, 20, 22, 23, 25, 26)
+TENSOR_CHUNKS = (6, 7)
+TENSOR_STEPS = range(6, 26, 2)
 VECTOR_ADDS_FROM = TILES - 1
 ONES_ROW = 64
 EPS = 1e-6
@@ -410,4 +410,4 @@ def tile_gemmaattention_pa_t_kernel(
                     flip(flips)
                     flips += 1
                 if t in TENSOR_STEPS:
-                    tensor_piece(TENSOR_STEPS.index(t))
+                    tensor_piece((t - TENSOR_STEPS.start) // TENSOR_STEPS.step)

@@ -31,12 +31,12 @@ TILES = S // P
 CHUNK = 4
 CHUNKS = TILES // CHUNK
 PAIR = 2
-FLIP_AHEAD = 7
+FLIP_AHEAD = 8
 X_CHUNKS_HELD = 4
 VECTOR_PIECES = 3
 VECTOR_SINE_TILES = 2
-TENSOR_CHUNKS = (6, 7)
-TENSOR_STEPS = range(6, 26, 2)
+TENSOR_TILES = {6: (2, 3), 7: (0, 1, 2, 3)}
+TENSOR_STEPS = range(8, 24, 2)
 VECTOR_ADDS_FROM = TILES - 1
 ONES_ROW = 64
 EPS = 1e-6
@@ -63,9 +63,8 @@ def tile_gemmaattention_pa_t_kernel(
         work = ctx.enter_context(tc.tile_pool(name="work", bufs=3))
         prods = ctx.enter_context(tc.tile_pool(name="prods", bufs=6))
         outs = ctx.enter_context(tc.tile_pool(name="outs", bufs=3))
-        psum_keep = ctx.enter_context(tc.psum_pool(name="psum_keep", bufs=1))
         psum_t = ctx.enter_context(tc.psum_pool(name="psum_t", bufs=2))
-        psum_acc = ctx.enter_context(tc.psum_pool(name="psum_acc", bufs=5))
+        psum_acc = ctx.enter_context(tc.psum_pool(name="psum_acc", bufs=6))
 
         x_sb = {}
         for c in range(X_CHUNKS_HELD):
@@ -82,9 +81,8 @@ def tile_gemmaattention_pa_t_kernel(
 
         warm_in = keep.tile([P, 1], F32)
         warm_out = keep.tile([P, 1], F32)
-        def load_trig(first, after):
-            nc.sync.dma_start(out=cos_sb[:, first:after, :], in_=cos_dram[:, first:after, :])
-            nc.sync.dma_start(out=sin_sb[:, first:after, :], in_=sin_dram[:, first:after, :])
+        def load_trig(sb, dram, first, after):
+            nc.sync.dma_start(out=sb[:, first:after, :], in_=dram[:, first:after, :])
 
         def load_x(c, first, after):
             nc.sync.dma_start(
@@ -162,34 +160,34 @@ def tile_gemmaattention_pa_t_kernel(
         turned_of = {}
 
         def turn_trig(c):
+            tiles = TENSOR_TILES[c]
             aux = psum_t.tile([P, 2 * CHUNK, P], BF16, name="flipped")
-            for i in range(CHUNK):
-                nc.tensor.transpose(aux[:, i, :], cos_sb[:, c * CHUNK + i, :], diag_ones[:, 0, 0, :])
-                nc.tensor.transpose(aux[:, CHUNK + i, :], sin_sb[:, c * CHUNK + i, :], diag_ones[:, 0, 0, :])
+            for n, (sb, i) in enumerate((sb, i) for sb in (cos_sb, sin_sb) for i in tiles):
+                nc.tensor.transpose(aux[:, n, :], sb[:, c * CHUNK + i, :], diag_ones[:, 0, 0, :])
             turned_of[c] = turned.tile([P, 2 * CHUNK, P], BF16, name="trig")
-            nc.scalar.copy(out=turned_of[c][:], in_=aux[:])
+            nc.scalar.copy(out=turned_of[c][:, 0 : 2 * len(tiles), :], in_=aux[:, 0 : 2 * len(tiles), :])
 
-        def make_table_on_tensor(c, i):
+        def make_table_on_tensor(c, n):
+            tiles = TENSOR_TILES[c]
             aux = psum_t.tile([P, 2, 4, HALF], F32, name="flipped")
             for f, slots in ((0, slice(0, 4, 3)), (1, slice(1, 3))):
                 for rhs, first in ((diag_ones, True), (diag_w, False)):
                     nc.tensor.matmul(
                         out=aux[:, :, slots, :],
-                        lhsT=turned_of[c][:, CHUNK * f + i, :],
+                        lhsT=turned_of[c][:, len(tiles) * f + n, :],
                         rhs=rhs[:, f, :, :].rearrange("p q (s j) -> p q s j", s=2),
                         start=first, stop=not first,
                     )
             nc.scalar.copy(
-                out=table_of[c][:, i, :, :, :].rearrange("p q a d -> p (q a d)"),
+                out=table_of[c][:, tiles[n], :, :, :].rearrange("p q a d -> p (q a d)"),
                 in_=aux[:].rearrange("p q s j -> p (q s j)"),
             )
 
-        def tensor_piece(n):
-            c = TENSOR_CHUNKS[n // (1 + CHUNK)]
-            if n % (1 + CHUNK) == 0:
-                turn_trig(c)
-            else:
-                make_table_on_tensor(c, n % (1 + CHUNK) - 1)
+        tensor_work = []
+        for c, tiles in TENSOR_TILES.items():
+            tensor_work.append((turn_trig, (c,)))
+            for n in range(len(tiles)):
+                tensor_work.append((make_table_on_tensor, (c, n)))
 
         groups = [(0, 1), (1, 1), (2, PAIR), (4, PAIR), (6, PAIR)] + [(c * CHUNK, CHUNK) for c in range(2, CHUNKS)]
         group_of = {}
@@ -340,23 +338,25 @@ def tile_gemmaattention_pa_t_kernel(
             nc.vector.memset(w_planes[:].bitcast(I32), 0)
             load_x(0, 0, 1)
             nc.sync.dma_start(out=w_rows[0:1, 0, :], in_=q_norm_w.unsqueeze(0))
+            load_trig(cos_sb, cos_dram, 0, CHUNK)
             nc.sync.dma_start(
                 out=w_words[:].bitcast(I32), in_=w_qkv_words.bitcast(I32).rearrange("g p b -> p g b")
             )
             scale_rows = w_qkv_scales.bitcast(I32).rearrange("g (q r) n -> r q g n", r=4)
             for r in range(4):
                 nc.sync.dma_start(out=w_planes[r:P:32, :, :].bitcast(I32), in_=scale_rows[r])
-            load_trig(0, CHUNK)
+            load_trig(sin_sb, sin_dram, 0, CHUNK)
+            load_trig(cos_sb, cos_dram, CHUNK, 3 * CHUNK)
             load_x(0, 1, PAIR)
-            load_trig(CHUNK, 3 * CHUNK)
+            load_trig(sin_sb, sin_dram, CHUNK, 3 * CHUNK)
             load_x(0, PAIR, CHUNK)
             load_x(1, 0, CHUNK)
-            load_trig(3 * CHUNK, TILES)
+            load_trig(cos_sb, cos_dram, 3 * CHUNK, TILES)
+            load_trig(sin_sb, sin_dram, 3 * CHUNK, TILES)
             for c in range(2, X_CHUNKS_HELD):
                 load_x(c, 0, CHUNK)
             flip(0)
-            quantise(0)
-            gain_ps = psum_keep.tile([P, 2, 2, D], F32, name="aux")
+            gain_ps = psum_acc.tile([P, 2, 2, D], F32, name="acc")
             gain_too = psum_t.tile([P, 2 * PASSES, P], F32, name="flipped")
             nc.tensor.matmul(out=gain_ps[:, 0, :, :], lhsT=pick[:], rhs=w_rows[:], start=True, stop=True)
             for gain_1 in (gain_ps[:, 1, :, :], gain_too[:, 0:2, :]):
@@ -368,27 +368,34 @@ def tile_gemmaattention_pa_t_kernel(
                 )
             gain_sb = keep.tile([P, 2, D], F32)
             nc.scalar.copy(out=gain_sb[:], in_=gain_too[:, 0:2, :])
-            make_tables(0)
+            vector_table(0, 0)
+            quantise(0)
+            vector_table(0, 2)
+            vector_table(0, 1)
             make_tables_on_gpsimd(0)
             multiply(0)
             make_diag_w()
+            vector_table(1, 0)
+            vector_table(1, 2)
+            make_tables_on_gpsimd(1)
             normalise(0)
             flip(1)
             rotate(0, between=lambda: quantise(1))
-            make_tables_on_gpsimd(1)
+            make_tables_on_gpsimd(2)
             flip(2)
             flip(3)
             multiply(1)
             quantise(3)
-            make_tables(1)
+            vector_table(1, 1)
+            make_tables(2)
             normalise(1)
             rotate(1)
             flip(4)
             flip(5)
-        quantise_after = {2: 4, 3: 6}
-        for c in range(2, CHUNKS):
-            quantise_after[c * CHUNK - 3] = c * CHUNK
-        table_work = [(c, piece) for c in range(2, CHUNKS) if c not in TENSOR_CHUNKS for piece in range(VECTOR_PIECES)]
+        quantise_after = {2: 4, 3: 6, 5: 8}
+        for c in range(3, CHUNKS):
+            quantise_after[(c - 1) * CHUNK] = c * CHUNK
+        table_work = [(c, piece) for c in range(3, 6) for piece in range(VECTOR_PIECES)] + [(6, 0), (6, 1)]
         flips = 6
         tables_done = 0
         with tc.manual_schedule(engines={EngineType.DVE}):
@@ -396,11 +403,11 @@ def tile_gemmaattention_pa_t_kernel(
                 multiply(t)
                 normalise(t)
                 if tables_done < len(table_work) and t not in quantise_after:
-                    c, piece = table_work[tables_done]
+                    c, part = table_work[tables_done]
                     tables_done += 1
-                    if piece == 0:
+                    if part == 0 and c not in TENSOR_TILES:
                         make_tables_on_gpsimd(c)
-                    rotate(t, between=lambda: vector_table(c, piece), between_at=NORMED - 1)
+                    rotate(t, between=lambda: vector_table(c, part), between_at=NORMED - 1)
                 else:
                     rotate(t)
                 if t in quantise_after:
@@ -410,4 +417,5 @@ def tile_gemmaattention_pa_t_kernel(
                     flip(flips)
                     flips += 1
                 if t in TENSOR_STEPS:
-                    tensor_piece((t - TENSOR_STEPS.start) // TENSOR_STEPS.step)
+                    piece, of = tensor_work[TENSOR_STEPS.index(t)]
+                    piece(*of)

@@ -31,7 +31,6 @@ TILES = S // P
 CHUNK = 4
 CHUNKS = TILES // CHUNK
 PAIR = 2
-FLIP_AHEAD = 8
 X_CHUNKS_HELD = 4
 VECTOR_PIECES = 3
 VECTOR_SINE_TILES = 2
@@ -413,9 +412,10 @@ def tile_gemmaattention_pa_t_kernel(
                 if t in quantise_after:
                     start = quantise_after[t]
                     quantise(start + group_of[start][1] - 1)
-                while flips < min(2 * t + 4, t + 1 + FLIP_AHEAD, TILES):
+                if flips < TILES and (t < 5 or t % 2 == 1):
                     flip(flips)
-                    flips += 1
+                    flip(flips + 1)
+                    flips += 2
                 if t in TENSOR_STEPS:
                     piece, of = tensor_work[TENSOR_STEPS.index(t)]
                     piece(*of)

@@ -32,11 +32,11 @@ CHUNK = 4
 CHUNKS = TILES // CHUNK
 PAIR = 2
 X_CHUNKS_HELD = 4
-VECTOR_PIECES = 3
-VECTOR_SINE_TILES = 2
+SINGLE_FROM = TILES - 4
+VECTOR_SINE_TILES = 1
 TENSOR_TILES = {6: (2, 3), 7: (0, 1, 2, 3)}
 TENSOR_STEPS = range(8, 24, 2)
-VECTOR_ADDS_FROM = TILES - 1
+VECTOR_ADDS_FROM = TILES - 2
 ONES_ROW = 64
 EPS = 1e-6
 
@@ -56,11 +56,11 @@ def tile_gemmaattention_pa_t_kernel(
 
     with ExitStack() as ctx:
         keep = ctx.enter_context(tc.tile_pool(name="keep", bufs=1))
-        tables = ctx.enter_context(tc.tile_pool(name="tables", bufs=CHUNKS))
+        tables = ctx.enter_context(tc.tile_pool(name="tables", bufs=6))
         xs = ctx.enter_context(tc.tile_pool(name="xs", bufs=X_CHUNKS_HELD))
         front = ctx.enter_context(tc.tile_pool(name="front", bufs=3))
         work = ctx.enter_context(tc.tile_pool(name="work", bufs=3))
-        prods = ctx.enter_context(tc.tile_pool(name="prods", bufs=6))
+        prods = ctx.enter_context(tc.tile_pool(name="prods", bufs=4))
         outs = ctx.enter_context(tc.tile_pool(name="outs", bufs=3))
         psum_t = ctx.enter_context(tc.psum_pool(name="psum_t", bufs=2))
         psum_acc = ctx.enter_context(tc.psum_pool(name="psum_acc", bufs=6))
@@ -109,32 +109,36 @@ def tile_gemmaattention_pa_t_kernel(
 
         mid = VECTOR_SINE_TILES
 
-        def slots_of(c):
-            return table_of[c][:].rearrange("p i q a (b j) -> p i q (a b) j", b=2)
+        def table(c):
+            if c not in table_of:
+                table_of[c] = tables.tile([P, CHUNK, 2, 2, D], F32, name="table")
+            return table_of[c]
 
-        def vector_table(c, piece):
-            first = 0 if piece < 2 else mid
-            ts = slice(c * CHUNK + first, c * CHUNK + first + mid)
-            if piece == 1:
-                nc.vector.tensor_tensor(
-                    out=slots_of(c)[:, 0:mid, :, 1:3, :].rearrange("p i q s j -> p i q (s j)"),
-                    in0=gain_ps[:, 1, :, :].unsqueeze(1).to_broadcast([P, mid, 2, D]),
-                    in1=sin_sb[:, ts, :].unsqueeze(2).to_broadcast([P, mid, 2, D]),
-                    op=ALU.mult,
-                )
-            else:
-                nc.vector.tensor_tensor(
-                    out=slots_of(c)[:, first : first + mid, :, 0:4:3, :],
-                    in0=gain_ps[:, 0, :, :].rearrange("p q (s j) -> p q s j", s=2)
-                    .unsqueeze(1).to_broadcast([P, mid, 2, 2, HALF]),
-                    in1=cos_sb[:, ts, :].rearrange("p i (s j) -> p i s j", s=2)
-                    .unsqueeze(2).to_broadcast([P, mid, 2, 2, HALF]),
-                    op=ALU.mult,
-                )
+        def slots_of(c):
+            return table(c)[:].rearrange("p i q a (b j) -> p i q (a b) j", b=2)
+
+        def vector_cosine(c, first):
+            nc.vector.tensor_tensor(
+                out=slots_of(c)[:, first : first + PAIR, :, 0:4:3, :],
+                in0=gain_ps[:, 0, :, :].rearrange("p q (s j) -> p q s j", s=2)
+                .unsqueeze(1).to_broadcast([P, PAIR, 2, 2, HALF]),
+                in1=cos_sb[:, c * CHUNK + first : c * CHUNK + first + PAIR, :]
+                .rearrange("p i (s j) -> p i s j", s=2).unsqueeze(2).to_broadcast([P, PAIR, 2, 2, HALF]),
+                op=ALU.mult,
+            )
+
+        def vector_sine(c, count=mid):
+            nc.vector.tensor_tensor(
+                out=slots_of(c)[:, 0:count, :, 1:3, :].rearrange("p i q s j -> p i q (s j)"),
+                in0=gain_ps[:, 1, :, :].unsqueeze(1).to_broadcast([P, count, 2, D]),
+                in1=sin_sb[:, c * CHUNK : c * CHUNK + count, :].unsqueeze(2).to_broadcast([P, count, 2, D]),
+                op=ALU.mult,
+            )
 
         def make_tables(c):
-            for piece in range(VECTOR_PIECES):
-                vector_table(c, piece)
+            vector_cosine(c, 0)
+            vector_sine(c)
+            vector_cosine(c, PAIR)
 
         def make_tables_on_gpsimd(c):
             nc.gpsimd.tensor_tensor(
@@ -178,7 +182,7 @@ def tile_gemmaattention_pa_t_kernel(
                         start=first, stop=not first,
                     )
             nc.scalar.copy(
-                out=table_of[c][:, tiles[n], :, :, :].rearrange("p q a d -> p (q a d)"),
+                out=table(c)[:, tiles[n], :, :, :].rearrange("p q a d -> p (q a d)"),
                 in_=aux[:].rearrange("p q s j -> p (q s j)"),
             )
 
@@ -259,18 +263,18 @@ def tile_gemmaattention_pa_t_kernel(
         def head_columns(banks, h):
             return banks[h // Q_HEADS][:, (h % Q_HEADS) * D : (h % Q_HEADS + 1) * D]
 
-        def add_halves(engine, prod, qk_out, i, first, after):
+        def add_halves(engine, prod, qk_out, first, after):
+            rows = prod[:].rearrange("p i r a d -> p (i r) a d")[:, first:after]
             engine.tensor_tensor(
-                out=qk_out[:, i * NORMED + first : i * NORMED + after, :].rearrange("p r (a j) -> p r a j", a=2),
-                in0=prod[:, first:after, :, 0:HALF],
-                in1=prod[:, first:after, :, HALF:D],
+                out=qk_out[:, first:after, :].rearrange("p r (a j) -> p r a j", a=2),
+                in0=rows[:, :, :, 0:HALF],
+                in1=rows[:, :, :, HALF:D],
                 op=ALU.add,
             )
 
-        for c in range(CHUNKS):
-            table_of[c] = tables.tile([P, CHUNK, 2, 2, D], F32, name="table")
         outs_of = {}
         rstd_of = {}
+        prod_of = {}
 
         def normalise(t):
             banks = banks_of[t]
@@ -300,12 +304,14 @@ def tile_gemmaattention_pa_t_kernel(
             i = t % PAIR
             qk_out, v_out = outs_of[t - i]
             by_tile = qk_out[:].rearrange("p (i h) d -> p i (h d)", h=NORMED)
-            prod = prods.tile([P, NORMED, 2, D], F32, name="prod")
+            if i == 0:
+                prod_of[t] = prods.tile([P, PAIR, NORMED, 2, D], F32, name="prod")
+            prod = prod_of[t - i]
             for h in range(NORMED):
                 if between is not None and h == between_at:
                     between()
                 nc.vector.scalar_tensor_tensor(
-                    out=prod[:, h, :, :],
+                    out=prod[:, i, h, :, :],
                     in0=head_columns(banks, h).unsqueeze(1).to_broadcast([P, 2, D]),
                     scalar=rstd[:, h : h + 1],
                     in1=table_of[t // CHUNK][:, t % CHUNK, h // Q_HEADS, :, :],
@@ -314,7 +320,10 @@ def tile_gemmaattention_pa_t_kernel(
                 )
             adder = nc.vector if t >= VECTOR_ADDS_FROM else nc.gpsimd
             if t < TILES - PAIR:
-                add_halves(adder, prod, qk_out, i, 0, NORMED)
+                if t >= SINGLE_FROM:
+                    add_halves(adder, prod, qk_out, i * NORMED, (i + 1) * NORMED)
+                elif i == PAIR - 1:
+                    add_halves(adder, prod, qk_out, 0, PAIR * NORMED)
                 if i == PAIR - 1:
                     ts = slice(t - PAIR + 1, t + 1)
                     nc.sync.dma_start(out=v_dram[:, ts, :], in_=v_out[:])
@@ -323,9 +332,9 @@ def tile_gemmaattention_pa_t_kernel(
             else:
                 ts = slice(t, t + 1)
                 nc.sync.dma_start(out=v_dram[:, ts, :], in_=v_out[:, i : i + 1, :])
-                add_halves(adder, prod, qk_out, i, 0, Q_HEADS)
+                add_halves(adder, prod, qk_out, i * NORMED, i * NORMED + Q_HEADS)
                 nc.sync.dma_start(out=q_dram[:, ts, :], in_=by_tile[:, i : i + 1, 0 : Q_HEADS * D])
-                add_halves(adder, prod, qk_out, i, Q_HEADS, NORMED)
+                add_halves(adder, prod, qk_out, i * NORMED + Q_HEADS, (i + 1) * NORMED)
                 nc.sync.dma_start(out=k_dram[:, ts, :], in_=by_tile[:, i : i + 1, Q_HEADS * D : NORMED * D])
 
         with tc.manual_schedule(engines={EngineType.SP, EngineType.PE, EngineType.Activation, EngineType.DVE}):
@@ -367,15 +376,15 @@ def tile_gemmaattention_pa_t_kernel(
                 )
             gain_sb = keep.tile([P, 2, D], F32)
             nc.scalar.copy(out=gain_sb[:], in_=gain_too[:, 0:2, :])
-            vector_table(0, 0)
+            vector_cosine(0, 0)
             quantise(0)
-            vector_table(0, 2)
-            vector_table(0, 1)
+            vector_cosine(0, PAIR)
+            vector_sine(0)
             make_tables_on_gpsimd(0)
             multiply(0)
             make_diag_w()
-            vector_table(1, 0)
-            vector_table(1, 2)
+            vector_cosine(1, 0)
+            vector_cosine(1, PAIR)
             make_tables_on_gpsimd(1)
             normalise(0)
             flip(1)
@@ -385,16 +394,20 @@ def tile_gemmaattention_pa_t_kernel(
             flip(3)
             multiply(1)
             quantise(3)
-            vector_table(1, 1)
+            vector_sine(1)
             make_tables(2)
             normalise(1)
             rotate(1)
             flip(4)
             flip(5)
-        quantise_after = {2: 4, 3: 6, 5: 8}
-        for c in range(3, CHUNKS):
-            quantise_after[(c - 1) * CHUNK] = c * CHUNK
-        table_work = [(c, piece) for c in range(3, 6) for piece in range(VECTOR_PIECES)] + [(6, 0), (6, 1)]
+            quantise(5)
+        quantise_after = {3: 6}
+        for c in range(2, CHUNKS):
+            quantise_after[c * CHUNK - 3] = c * CHUNK
+        table_work = []
+        for c in range(3, 6):
+            table_work += [(vector_cosine, (c, 0)), (vector_sine, (c,)), (vector_cosine, (c, PAIR))]
+        table_work += [(vector_cosine, (6, 0)), (vector_sine, (6, PAIR))]
         flips = 6
         tables_done = 0
         with tc.manual_schedule(engines={EngineType.DVE}):
@@ -402,11 +415,11 @@ def tile_gemmaattention_pa_t_kernel(
                 multiply(t)
                 normalise(t)
                 if tables_done < len(table_work) and t not in quantise_after:
-                    c, part = table_work[tables_done]
+                    make, what = table_work[tables_done]
                     tables_done += 1
-                    if part == 0 and c not in TENSOR_TILES:
-                        make_tables_on_gpsimd(c)
-                    rotate(t, between=lambda: vector_table(c, part), between_at=NORMED - 1)
+                    if what[0] not in TENSOR_TILES and what[1:] == (0,):
+                        make_tables_on_gpsimd(what[0])
+                    rotate(t, between=lambda: make(*what), between_at=NORMED - 1)
                 else:
                     rotate(t)
                 if t in quantise_after:

@@ -318,23 +318,23 @@ def tile_gemmaattention_pa_t_kernel(
                     op0=ALU.mult,
                     op1=ALU.mult,
                 )
-            adder = nc.vector if t >= VECTOR_ADDS_FROM else nc.gpsimd
-            if t < TILES - PAIR:
-                if t >= SINGLE_FROM:
-                    add_halves(adder, prod, qk_out, i * NORMED, (i + 1) * NORMED)
-                elif i == PAIR - 1:
-                    add_halves(adder, prod, qk_out, 0, PAIR * NORMED)
+            if t < SINGLE_FROM:
                 if i == PAIR - 1:
                     ts = slice(t - PAIR + 1, t + 1)
+                    add_halves(nc.gpsimd, prod, qk_out, 0, PAIR * NORMED)
                     nc.sync.dma_start(out=v_dram[:, ts, :], in_=v_out[:])
                     nc.sync.dma_start(out=q_dram[:, ts, :], in_=by_tile[:, :, 0 : Q_HEADS * D])
                     nc.sync.dma_start(out=k_dram[:, ts, :], in_=by_tile[:, :, Q_HEADS * D : NORMED * D])
             else:
                 ts = slice(t, t + 1)
+                first, middle, after = i * NORMED, i * NORMED + Q_HEADS, (i + 1) * NORMED
                 nc.sync.dma_start(out=v_dram[:, ts, :], in_=v_out[:, i : i + 1, :])
-                add_halves(adder, prod, qk_out, i * NORMED, i * NORMED + Q_HEADS)
+                if t < VECTOR_ADDS_FROM:
+                    add_halves(nc.gpsimd, prod, qk_out, first, after)
+                else:
+                    add_halves(nc.vector, prod, qk_out, first, middle)
+                    add_halves(nc.vector, prod, qk_out, middle, after)
                 nc.sync.dma_start(out=q_dram[:, ts, :], in_=by_tile[:, i : i + 1, 0 : Q_HEADS * D])
-                add_halves(adder, prod, qk_out, i * NORMED + Q_HEADS, (i + 1) * NORMED)
                 nc.sync.dma_start(out=k_dram[:, ts, :], in_=by_tile[:, i : i + 1, Q_HEADS * D : NORMED * D])
 
         with tc.manual_schedule(engines={EngineType.SP, EngineType.PE, EngineType.Activation, EngineType.DVE}):

from contextlib import ExitStack

import concourse.mybir as mybir
from concourse.masks import make_identity

F32 = mybir.dt.float32
BF16 = mybir.dt.bfloat16
I32 = mybir.dt.int32
U8 = mybir.dt.uint8
U32 = mybir.dt.uint32
FP8X4 = mybir.dt.float8_e4m3fn_x4
FP4X4 = mybir.dt.float4_e2m1fn_x4
ALU = mybir.AluOpType
ACT = mybir.ActivationFunctionType
EngineType = mybir.EngineType

P = 128
S = 4096
HID = 1024
D = 128
HALF = D // 2
Q_HEADS = 4
K_HEADS = 2
V_HEADS = 2
NORMED = Q_HEADS + K_HEADS
N_OUT = (Q_HEADS + K_HEADS + V_HEADS) * D
N_PASS = 512
K_PASS = 512
PASSES = HID // K_PASS
TILES = S // P
CHUNK = 4
CHUNKS = TILES // CHUNK
PAIR = 2
X_CHUNKS_HELD = 4
SINGLE_FROM = TILES - 4
VECTOR_SINE_TILES = 1
TENSOR_TILES = {6: (2, 3), 7: (0, 1, 2, 3)}
TENSOR_STEPS = range(8, 24, 2)
VECTOR_ADDS_FROM = TILES - 2
ONES_ROW = 64
EPS = 1e-6

FLOPS = 2 * S * HID * N_OUT


def tile_gemmaattention_pa_t_kernel(
    tc, hidden_states, w_qkv_words, w_qkv_scales, q_norm_w, k_norm_w, cos, sin, out_0, out_1, out_2
):
    nc = tc.nc
    x_dram = hidden_states.rearrange("(p t) k -> p t k", t=TILES)
    cos_dram = cos.rearrange("(p t) d -> p t d", t=TILES)
    sin_dram = sin.rearrange("(p t) d -> p t d", t=TILES)
    q_dram = out_0.rearrange("(p t) h d -> p t (h d)", t=TILES)
    k_dram = out_1.rearrange("(p t) h d -> p t (h d)", t=TILES)
    v_dram = out_2.rearrange("(p t) h d -> p t (h d)", t=TILES)

    with ExitStack() as ctx:
        keep = ctx.enter_context(tc.tile_pool(name="keep", bufs=1))
        tables = ctx.enter_context(tc.tile_pool(name="tables", bufs=6))
        xs = ctx.enter_context(tc.tile_pool(name="xs", bufs=X_CHUNKS_HELD))
        front = ctx.enter_context(tc.tile_pool(name="front", bufs=3))
        work = ctx.enter_context(tc.tile_pool(name="work", bufs=3))
        prods = ctx.enter_context(tc.tile_pool(name="prods", bufs=4))
        outs = ctx.enter_context(tc.tile_pool(name="outs", bufs=3))
        psum_t = ctx.enter_context(tc.psum_pool(name="psum_t", bufs=2))
        psum_acc = ctx.enter_context(tc.psum_pool(name="psum_acc", bufs=6))

        x_sb = {}
        for c in range(X_CHUNKS_HELD):
            x_sb[c] = xs.tile([P, CHUNK, HID], BF16, name="x")
        w_planes = keep.tile([P, PASSES, N_OUT], U8, align_bytes=64)
        w_words = keep.tile([P, PASSES, 2 * N_OUT], U8, align_bytes=64)
        cos_sb = keep.tile([P, TILES, D], BF16)
        sin_sb = keep.tile([P, TILES, D], BF16)
        w_rows = keep.tile([P, 2, D], BF16)
        signs = keep.tile([P, 2, 2, D], BF16)
        diag_ones = keep.tile([P, 2, 2, D], BF16)
        diag_w = keep.tile([P, 2, 2, D], BF16)
        turned = ctx.enter_context(tc.tile_pool(name="turned", bufs=2))

        warm_in = keep.tile([P, 1], F32)
        warm_out = keep.tile([P, 1], F32)
        def load_trig(sb, dram, first, after):
            nc.sync.dma_start(out=sb[:, first:after, :], in_=dram[:, first:after, :])

        def load_x(c, first, after):
            nc.sync.dma_start(
                out=x_sb[c][:, first:after, :], in_=x_dram[:, c * CHUNK + first : c * CHUNK + after, :]
            )

        pick = keep.tile([P, P], BF16)
        pick_minus = keep.tile([P, P], BF16)
        for tile, value in ((pick, 1.0), (pick_minus, -1.0)):
            nc.gpsimd.memset(tile[:], 0.0)
            nc.gpsimd.memset(tile[0:1, :], value)
            nc.gpsimd.memset(tile[ONES_ROW : ONES_ROW + 1, :], value)
        ident = keep.tile([P, P], F32)
        make_identity(nc, ident[:])
        nc.gpsimd.memset(signs[:], 1.0)
        nc.gpsimd.memset(signs[:, 1, :, 0:HALF], -1.0)
        nc.gpsimd.tensor_tensor(
            out=diag_ones[:].rearrange("p c q d -> p (c q) d"),
            in0=signs[:].rearrange("p c q d -> p (c q) d"),
            in1=ident[:].unsqueeze(1).to_broadcast([P, 4, D]),
            op=ALU.mult,
        )

        table_of = {}

        mid = VECTOR_SINE_TILES

        def table(c):
            if c not in table_of:
                table_of[c] = tables.tile([P, CHUNK, 2, 2, D], F32, name="table")
            return table_of[c]

        def slots_of(c):
            return table(c)[:].rearrange("p i q a (b j) -> p i q (a b) j", b=2)

        def vector_cosine(c, first):
            nc.vector.tensor_tensor(
                out=slots_of(c)[:, first : first + PAIR, :, 0:4:3, :],
                in0=gain_ps[:, 0, :, :].rearrange("p q (s j) -> p q s j", s=2)
                .unsqueeze(1).to_broadcast([P, PAIR, 2, 2, HALF]),
                in1=cos_sb[:, c * CHUNK + first : c * CHUNK + first + PAIR, :]
                .rearrange("p i (s j) -> p i s j", s=2).unsqueeze(2).to_broadcast([P, PAIR, 2, 2, HALF]),
                op=ALU.mult,
            )

        def vector_sine(c, count=mid):
            nc.vector.tensor_tensor(
                out=slots_of(c)[:, 0:count, :, 1:3, :].rearrange("p i q s j -> p i q (s j)"),
                in0=gain_ps[:, 1, :, :].unsqueeze(1).to_broadcast([P, count, 2, D]),
                in1=sin_sb[:, c * CHUNK : c * CHUNK + count, :].unsqueeze(2).to_broadcast([P, count, 2, D]),
                op=ALU.mult,
            )

        def make_tables(c):
            vector_cosine(c, 0)
            vector_sine(c)
            vector_cosine(c, PAIR)

        def make_tables_on_gpsimd(c):
            nc.gpsimd.tensor_tensor(
                out=slots_of(c)[:, mid:CHUNK, :, 1:3, :].rearrange("p i q s j -> p i q (s j)"),
                in0=gain_sb[:].unsqueeze(1).to_broadcast([P, CHUNK - mid, 2, D]),
                in1=sin_sb[:, c * CHUNK + mid : (c + 1) * CHUNK, :]
                .unsqueeze(2).to_broadcast([P, CHUNK - mid, 2, D]),
                op=ALU.mult,
            )

        def make_diag_w():
            for c, first, after, one in ((0, 0, D, -1.0), (1, 0, HALF, 1.0), (1, HALF, D, -1.0)):
                nc.vector.scalar_tensor_tensor(
                    out=diag_w[:, c, :, first:after],
                    in0=gain_ps[:, c, :, first:after],
                    scalar=one,
                    in1=ident[:, first:after].unsqueeze(1).to_broadcast([P, 2, after - first]),
                    op0=ALU.add,
                    op1=ALU.mult,
                )

        turned_of = {}

        def turn_trig(c):
            tiles = TENSOR_TILES[c]
            aux = psum_t.tile([P, 2 * CHUNK, P], BF16, name="flipped")
            for n, (sb, i) in enumerate((sb, i) for sb in (cos_sb, sin_sb) for i in tiles):
                nc.tensor.transpose(aux[:, n, :], sb[:, c * CHUNK + i, :], diag_ones[:, 0, 0, :])
            turned_of[c] = turned.tile([P, 2 * CHUNK, P], BF16, name="trig")
            nc.scalar.copy(out=turned_of[c][:, 0 : 2 * len(tiles), :], in_=aux[:, 0 : 2 * len(tiles), :])

        def make_table_on_tensor(c, n):
            tiles = TENSOR_TILES[c]
            aux = psum_t.tile([P, 2, 4, HALF], F32, name="flipped")
            for f, slots in ((0, slice(0, 4, 3)), (1, slice(1, 3))):
                for rhs, first in ((diag_ones, True), (diag_w, False)):
                    nc.tensor.matmul(
                        out=aux[:, :, slots, :],
                        lhsT=turned_of[c][:, len(tiles) * f + n, :],
                        rhs=rhs[:, f, :, :].rearrange("p q (s j) -> p q s j", s=2),
                        start=first, stop=not first,
                    )
            nc.scalar.copy(
                out=table(c)[:, tiles[n], :, :, :].rearrange("p q a d -> p (q a d)"),
                in_=aux[:].rearrange("p q s j -> p (q s j)"),
            )

        tensor_work = []
        for c, tiles in TENSOR_TILES.items():
            tensor_work.append((turn_trig, (c,)))
            for n in range(len(tiles)):
                tensor_work.append((make_table_on_tensor, (c, n)))

        groups = [(0, 1), (1, 1), (2, PAIR), (4, PAIR), (6, PAIR)] + [(c * CHUNK, CHUNK) for c in range(2, CHUNKS)]
        group_of = {}
        for start, count in groups:
            for t in range(start, start + count):
                group_of[t] = (start, count)
        grouped_of = {}
        codes_of = {}
        planes_of = {}

        def flip(t):
            start, count = group_of[t]
            if t == start:
                grouped_of[start] = front.tile(
                    [P, count, PASSES * P * 4], BF16, name="grouped", align_bytes=64
                )
            x_words = x_sb[t // CHUNK][:, t % CHUNK, :].bitcast(F32)
            flipped = psum_t.tile([P, 2 * PASSES, P], F32, name="flipped")
            for g in range(PASSES):
                for u in range(2):
                    nc.tensor.transpose(
                        flipped[:, 2 * g + u, :],
                        x_words[:, 256 * g + u : 256 * (g + 1) : 2],
                        ident[:],
                    )
            nc.scalar.copy(
                out=grouped_of[start][:, t - start, :]
                .bitcast(F32)
                .rearrange("p (g m u) -> p g m u", g=PASSES, u=2),
                in_=flipped[:].rearrange("p (g u) m -> p g m u", u=2),
            )
            if t % CHUNK == CHUNK - 1 and t // CHUNK + X_CHUNKS_HELD < CHUNKS:
                c = t // CHUNK + X_CHUNKS_HELD
                x_sb[c] = xs.tile([P, CHUNK, HID], BF16, name="x")
                load_x(c, 0, CHUNK)

        def quantise(t):
            start, count = group_of[t]
            if t == start + count - 1:
                codes_of[start] = front.tile([P, count, PASSES * P], U32, name="codes", align_bytes=64)
                planes_of[start] = front.tile([P, count, PASSES * P], U8, name="planes", align_bytes=64)
                nc.vector.quantize_mx(
                    out=codes_of[start][:].rearrange("p i c -> p (i c)").bitcast(FP8X4),
                    scales=planes_of[start][:].rearrange("p i c -> p (i c)"),
                    in_=grouped_of[start][:].rearrange("p i c -> p (i c)"),
                )

        banks_of = {}

        def multiply(t):
            start = group_of[t][0]
            codes = codes_of[start][:, t - start, :]
            planes = planes_of[start][:, t - start, :]
            banks = []
            for n in range(N_OUT // N_PASS):
                acc = psum_acc.tile([P, N_PASS], F32, name="acc")
                for g in range(PASSES):
                    nc.tensor.matmul_mx(
                        out=acc[:],
                        lhsT=codes[:, g * P : (g + 1) * P].bitcast(FP8X4),
                        lhsT_scale=planes[:, g * P : (g + 1) * P],
                        rhs=w_words[:, g, 2 * n * N_PASS : 2 * (n + 1) * N_PASS].bitcast(FP4X4),
                        rhs_scale=w_planes[:, g, n * N_PASS : (n + 1) * N_PASS],
                        start=(g == 0),
                        stop=(g == PASSES - 1),
                    )
                banks.append(acc)
            banks_of[t] = banks

        def head_columns(banks, h):
            return banks[h // Q_HEADS][:, (h % Q_HEADS) * D : (h % Q_HEADS + 1) * D]

        def add_halves(engine, prod, qk_out, first, after):
            rows = prod[:].rearrange("p i r a d -> p (i r) a d")[:, first:after]
            engine.tensor_tensor(
                out=qk_out[:, first:after, :].rearrange("p r (a j) -> p r a j", a=2),
                in0=rows[:, :, :, 0:HALF],
                in1=rows[:, :, :, HALF:D],
                op=ALU.add,
            )

        outs_of = {}
        rstd_of = {}
        prod_of = {}

        def normalise(t):
            banks = banks_of[t]
            i = t % PAIR
            if i == 0:
                qk_out = outs.tile([P, PAIR * NORMED, D], F32, name="qk_out")
                v_out = outs.tile([P, PAIR, V_HEADS * D], F32, name="v_out")
                outs_of[t] = (qk_out, v_out)
            v_out = outs_of[t - i][1]
            squares = work.tile([P, NORMED, D], BF16, name="squares")
            sumsq = work.tile([P, NORMED], F32, name="sumsq")
            for h in range(NORMED):
                nc.scalar.activation(
                    out=squares[:, h, :], in_=head_columns(banks, h), func=ACT.Square,
                    accum_out=sumsq[:, h : h + 1],
                )
            rstd = work.tile([P, NORMED], F32, name="rstd")
            nc.scalar.activation(
                out=rstd[:], in_=sumsq[:], func=ACT.Abs_reciprocal_sqrt, scale=1.0 / D, bias=EPS
            )
            rstd_of[t] = rstd
            nc.scalar.copy(out=v_out[:, i, :], in_=banks[1][:, K_HEADS * D : N_PASS])

        def rotate(t, between=None, between_at=NORMED // 2):
            banks = banks_of[t]
            rstd = rstd_of[t]
            i = t % PAIR
            qk_out, v_out = outs_of[t - i]
            by_tile = qk_out[:].rearrange("p (i h) d -> p i (h d)", h=NORMED)
            if i == 0:
                prod_of[t] = prods.tile([P, PAIR, NORMED, 2, D], F32, name="prod")
            prod = prod_of[t - i]
            for h in range(NORMED):
                if between is not None and h == between_at:
                    between()
                nc.vector.scalar_tensor_tensor(
                    out=prod[:, i, h, :, :],
                    in0=head_columns(banks, h).unsqueeze(1).to_broadcast([P, 2, D]),
                    scalar=rstd[:, h : h + 1],
                    in1=table_of[t // CHUNK][:, t % CHUNK, h // Q_HEADS, :, :],
                    op0=ALU.mult,
                    op1=ALU.mult,
                )
            if t < SINGLE_FROM:
                if i == PAIR - 1:
                    ts = slice(t - PAIR + 1, t + 1)
                    add_halves(nc.gpsimd, prod, qk_out, 0, PAIR * NORMED)
                    nc.sync.dma_start(out=v_dram[:, ts, :], in_=v_out[:])
                    nc.sync.dma_start(out=q_dram[:, ts, :], in_=by_tile[:, :, 0 : Q_HEADS * D])
                    nc.sync.dma_start(out=k_dram[:, ts, :], in_=by_tile[:, :, Q_HEADS * D : NORMED * D])
            else:
                ts = slice(t, t + 1)
                first, middle, after = i * NORMED, i * NORMED + Q_HEADS, (i + 1) * NORMED
                nc.sync.dma_start(out=v_dram[:, ts, :], in_=v_out[:, i : i + 1, :])
                if t < VECTOR_ADDS_FROM:
                    add_halves(nc.gpsimd, prod, qk_out, first, after)
                else:
                    add_halves(nc.vector, prod, qk_out, first, middle)
                    add_halves(nc.vector, prod, qk_out, middle, after)
                nc.sync.dma_start(out=q_dram[:, ts, :], in_=by_tile[:, i : i + 1, 0 : Q_HEADS * D])
                nc.sync.dma_start(out=k_dram[:, ts, :], in_=by_tile[:, i : i + 1, Q_HEADS * D : NORMED * D])

        with tc.manual_schedule(engines={EngineType.SP, EngineType.PE, EngineType.Activation, EngineType.DVE}):
            nc.gpsimd.memset(warm_in[:], 1.0)
            nc.vector.memset(w_rows[:], 0.0)
            nc.vector.memset(w_rows[ONES_ROW : ONES_ROW + 1, :, :], 1.0)
            nc.scalar.dma_start(out=w_rows[0:1, 1, :], in_=k_norm_w.unsqueeze(0))
            nc.scalar.activation(out=warm_out[:], in_=warm_in[:], func=ACT.Abs_reciprocal_sqrt)
            nc.vector.memset(w_planes[:].bitcast(I32), 0)
            load_x(0, 0, 1)
            nc.sync.dma_start(out=w_rows[0:1, 0, :], in_=q_norm_w.unsqueeze(0))
            load_trig(cos_sb, cos_dram, 0, CHUNK)
            nc.sync.dma_start(
                out=w_words[:].bitcast(I32), in_=w_qkv_words.bitcast(I32).rearrange("g p b -> p g b")
            )
            scale_rows = w_qkv_scales.bitcast(I32).rearrange("g (q r) n -> r q g n", r=4)
            for r in range(4):
                nc.sync.dma_start(out=w_planes[r:P:32, :, :].bitcast(I32), in_=scale_rows[r])
            load_trig(sin_sb, sin_dram, 0, CHUNK)
            load_trig(cos_sb, cos_dram, CHUNK, 3 * CHUNK)
            load_x(0, 1, PAIR)
            load_trig(sin_sb, sin_dram, CHUNK, 3 * CHUNK)
            load_x(0, PAIR, CHUNK)
            load_x(1, 0, CHUNK)
            load_trig(cos_sb, cos_dram, 3 * CHUNK, TILES)
            load_trig(sin_sb, sin_dram, 3 * CHUNK, TILES)
            for c in range(2, X_CHUNKS_HELD):
                load_x(c, 0, CHUNK)
            flip(0)
            gain_ps = psum_acc.tile([P, 2, 2, D], F32, name="acc")
            gain_too = psum_t.tile([P, 2 * PASSES, P], F32, name="flipped")
            nc.tensor.matmul(out=gain_ps[:, 0, :, :], lhsT=pick[:], rhs=w_rows[:], start=True, stop=True)
            for gain_1 in (gain_ps[:, 1, :, :], gain_too[:, 0:2, :]):
                nc.tensor.matmul(
                    out=gain_1[:, :, 0:HALF], lhsT=pick_minus[:], rhs=w_rows[:, :, HALF:D], start=True, stop=True
                )
                nc.tensor.matmul(
                    out=gain_1[:, :, HALF:D], lhsT=pick[:], rhs=w_rows[:, :, 0:HALF], start=True, stop=True
                )
            gain_sb = keep.tile([P, 2, D], F32)
            nc.scalar.copy(out=gain_sb[:], in_=gain_too[:, 0:2, :])
            vector_cosine(0, 0)
            quantise(0)
            vector_cosine(0, PAIR)
            vector_sine(0)
            make_tables_on_gpsimd(0)
            multiply(0)
            make_diag_w()
            vector_cosine(1, 0)
            vector_cosine(1, PAIR)
            make_tables_on_gpsimd(1)
            normalise(0)
            flip(1)
            rotate(0, between=lambda: quantise(1))
            make_tables_on_gpsimd(2)
            flip(2)
            flip(3)
            multiply(1)
            quantise(3)
            vector_sine(1)
            make_tables(2)
            normalise(1)
            rotate(1)
            flip(4)
            flip(5)
            quantise(5)
        quantise_after = {3: 6}
        for c in range(2, CHUNKS):
            quantise_after[c * CHUNK - 3] = c * CHUNK
        table_work = []
        for c in range(3, 6):
            table_work += [(vector_cosine, (c, 0)), (vector_sine, (c,)), (vector_cosine, (c, PAIR))]
        table_work += [(vector_cosine, (6, 0)), (vector_sine, (6, PAIR))]
        flips = 6
        tables_done = 0
        with tc.manual_schedule(engines={EngineType.DVE}):
            for t in range(2, TILES):
                multiply(t)
                normalise(t)
                if tables_done < len(table_work) and t not in quantise_after:
                    make, what = table_work[tables_done]
                    tables_done += 1
                    if what[0] not in TENSOR_TILES and what[1:] == (0,):
                        make_tables_on_gpsimd(what[0])
                    rotate(t, between=lambda: make(*what), between_at=NORMED - 1)
                else:
                    rotate(t)
                if t in quantise_after:
                    start = quantise_after[t]
                    quantise(start + group_of[start][1] - 1)
                if flips < TILES and (t < 5 or t % 2 == 1):
                    flip(flips)
                    flip(flips + 1)
                    flips += 2
                if t in TENSOR_STEPS:
                    piece, of = tensor_work[TENSOR_STEPS.index(t)]
                    piece(*of)
